import numpy as np
import ml_dtypes


def mxq(x, axis, fmt="e4m3"):
    dtype, down = {"e4m3": (ml_dtypes.float8_e4m3fn, 7), "e5m2": (ml_dtypes.float8_e5m2, 14)}[fmt]
    v = np.moveaxis(np.asarray(x, np.float32).astype(ml_dtypes.bfloat16).astype(np.float64), axis, -1)
    blocks = v.reshape(v.shape[:-1] + (-1, 32))
    amax = np.abs(blocks).max(-1, keepdims=True)
    byte = np.maximum(np.where(amax > 0, np.frexp(amax)[1] - 1 + 127, 0) - down, 1)
    scale = np.exp2(byte - 127.0)
    codes = (blocks / scale).astype(np.float32).astype(dtype).astype(np.float64)
    return np.moveaxis((codes * scale).reshape(v.shape), -1, axis)


WIDE = False


def mx_kscale(k):
    if not WIDE:
        return np.ones(k)
    levels = np.array([10, -10, 5, -5, 0])
    a = np.random.permutation(np.resize(levels, k // 512 * 4)).reshape(k // 512, 4)
    idx = np.arange(k)
    return np.exp2(a[idx // 512, idx % 128 // 32])


BF16 = ml_dtypes.bfloat16


def bf(x):
    return np.asarray(x, np.float32).astype(BF16)


def f64(x):
    return np.asarray(x).astype(np.float64)


B, N, D, H = 2, 2048, 512, 512
EDGE_P = 0.01
DEG = 1.0 + EDGE_P * N


def normalize_adj(adj):
    rowsum = adj.sum(axis=1)
    d_inv_sqrt = np.where(rowsum > 0, 1.0 / np.sqrt(np.maximum(rowsum, 1e-30)), 0.0)
    return d_inv_sqrt[:, :, None] * adj.transpose(0, 2, 1) * d_inv_sqrt[:, None, :]


def setup_inputs():
    s = mx_kscale(D)
    adj = (np.random.uniform(size=(B, N, N)) < EDGE_P).astype(np.float64)
    adj = np.minimum(adj + np.eye(N)[None], 1.0)
    return {"batch_graph": bf(np.random.standard_normal((B, N, D)) * s),
            "adj": bf(adj),
            "W1": bf(np.random.standard_normal((D, H)) * np.sqrt(DEG / D) / s[:, None]),
            "b1": bf(np.random.standard_normal(H) * 0.2)}


def reference(batch_graph, adj, W1, b1):
    a = normalize_adj(f64(adj))
    z = mxq(f64(batch_graph), 2, "e4m3") @ mxq(f64(W1), 0, "e4m3")
    return np.maximum((mxq(a, 2, "e4m3") @ mxq(z, 1, "e4m3")) + f64(b1), 0.0)

@@ -1,0 +1,286 @@
+from contextlib import ExitStack
+
+import concourse.mybir as mybir
+from concourse.masks import make_identity
+
+F32 = mybir.dt.float32
+BF16 = mybir.dt.bfloat16
+U32 = mybir.dt.uint32
+U8 = mybir.dt.uint8
+FP8X4 = mybir.dt.float8_e4m3fn_x4
+ALU = mybir.AluOpType
+ACT = mybir.ActivationFunctionType
+
+P = 128
+PACK = 4
+K_PASS = P * PACK
+
+GRAPHS, NODES, FEATS, HIDDEN = 2, 2048, 512, 512
+CHUNKS = NODES // P
+PASSES = NODES // K_PASS
+BLOCK = 512
+BLOCKS = NODES // BLOCK
+ROW_TILES = BLOCK // P
+ONES_N = 8
+STEPS = BLOCKS * PASSES
+HALF = CHUNKS // 2
+DEGREE_PIECES = 2 * PASSES + 4
+
+FLOPS = 2 * GRAPHS * NODES * FEATS * HIDDEN + 2 * GRAPHS * NODES * NODES * HIDDEN
+
+
+def side_by_side(copy, grouped, planes):
+    copy(
+        out=grouped.rearrange("p (c i) t -> p c t i", i=4),
+        in_=planes.rearrange("p t (c i) -> p c t i", i=4),
+    )
+
+
+def tile_perception_pa_kernel(tc, batch_graph, adj, W1, b1, out):
+    nc = tc.nc
+    with ExitStack() as ctx:
+        ctx.enter_context(tc.manual_schedule())
+        keep = ctx.enter_context(tc.tile_pool(name="keep", bufs=1))
+        work = ctx.enter_context(tc.psum_pool(name="work", bufs=4))
+        sums = ctx.enter_context(tc.psum_pool(name="sums", bufs=ROW_TILES))
+
+        ident = keep.tile([P, P], F32)
+        make_identity(nc, ident[:])
+        ones = keep.tile([P, P], BF16)
+        nc.vector.memset(ones[:], 1.0)
+        warm = keep.tile([P, 1], F32)
+        nc.vector.memset(warm[:], 1.0)
+        nc.scalar.activation(out=warm[:], in_=warm[:], func=ACT.Sqrt)
+
+        adj_sb = [
+            [keep.tile([P, PACK, NODES], BF16, name="adj%d_%d" % (b, g)) for g in range(PASSES)]
+            for b in range(GRAPHS)
+        ]
+        z_codes = [
+            keep.tile([P, PASSES, HIDDEN], U32, align_bytes=64, name="z_codes%d" % b)
+            for b in range(GRAPHS)
+        ]
+        z_scales = [
+            keep.tile([P, PASSES, HIDDEN], U8, align_bytes=64, name="z_scales%d" % b)
+            for b in range(GRAPHS)
+        ]
+        d_col = [keep.tile([P, CHUNKS], F32, name="d_col%d" % b) for b in range(GRAPHS)]
+        d_row = [keep.tile([P, NODES], F32, name="d_row%d" % b) for b in range(GRAPHS)]
+        bias_row = keep.tile([P, HIDDEN], F32)
+
+        with ExitStack() as stage1:
+            feats = stage1.enter_context(tc.tile_pool(name="feats", bufs=1))
+            rows1 = stage1.enter_context(tc.tile_pool(name="rows1", bufs=2))
+
+            w_planes = feats.tile([P, PACK, HIDDEN], BF16)
+            for u in range(2):
+                nc.sync.dma_start(
+                    out=w_planes[:, 2 * u : 2 * u + 2, :],
+                    in_=W1[256 * u : 256 * u + 256, :].rearrange("(q e) c -> q e c", e=2),
+                )
+            x_sb = {}
+            for b in range(GRAPHS):
+                x_chunks = batch_graph[b].rearrange("(r p) k -> p r k", p=P)
+                for g in range(PASSES):
+                    x_sb[b, g] = feats.tile([P, PACK, FEATS], BF16, name="x%d_%d" % (b, g))
+                    nc.sync.dma_start(out=x_sb[b, g][:], in_=x_chunks[:, PACK * g : PACK * (g + 1), :])
+            bias_in = feats.tile([P, HIDDEN], BF16)
+            nc.vector.memset(bias_in[:], 0.0)
+            nc.sync.dma_start(out=bias_in[0:1, :], in_=b1.rearrange("(o h) -> o h", o=1))
+            for b in range(GRAPHS):
+                adj_chunks = adj[b].rearrange("(r p) i -> p r i", p=P)
+                for g in range(PASSES):
+                    nc.sync.dma_start(out=adj_sb[b][g][:], in_=adj_chunks[:, PACK * g : PACK * (g + 1), :])
+
+            w_grouped = feats.tile([P, HIDDEN, PACK], BF16, align_bytes=64)
+            side_by_side(nc.vector.tensor_copy, w_grouped[:], w_planes[:])
+            w_codes = feats.tile([P, HIDDEN], U32, align_bytes=64)
+            w_scales = feats.tile([P, HIDDEN], U8, align_bytes=64)
+            nc.vector.quantize_mx(
+                out=w_codes[:].bitcast(FP8X4),
+                scales=w_scales[:],
+                in_=w_grouped[:].rearrange("p c t -> p (c t)"),
+            )
+
+            x_codes = {}
+            x_scales = {}
+
+            def features_to_codes(b, g):
+                x_words = x_sb[b, g][:].bitcast(F32)
+                x_grouped = rows1.tile([P, K_PASS, PACK], BF16, align_bytes=64)
+                x_grouped_words = x_grouped[:].bitcast(F32)
+                for half in range(2):
+                    xt = work.tile([P, 2, 2, P], F32, tag="work")
+                    for c in range(2):
+                        for u in range(2):
+                            nc.tensor.transpose(
+                                xt[:, c, u, :],
+                                x_words[:, 2 * half + c, P * u : P * (u + 1)],
+                                ident[:],
+                            )
+                    nc.scalar.copy(
+                        out=x_grouped_words[:, 2 * P * half : 2 * P * (half + 1), :].rearrange(
+                            "p (c n) u -> p c n u", c=2
+                        ),
+                        in_=xt[:].rearrange("p c u n -> p c n u"),
+                    )
+                x_codes[b, g] = rows1.tile([P, K_PASS], U32, align_bytes=64, name="x_codes")
+                x_scales[b, g] = rows1.tile([P, K_PASS], U8, align_bytes=64, name="x_scales")
+                nc.vector.quantize_mx(
+                    out=x_codes[b, g][:].bitcast(FP8X4),
+                    scales=x_scales[b, g][:],
+                    in_=x_grouped[:].rearrange("p n t -> p (n t)"),
+                )
+
+            def project(b, g):
+                z_grouped = rows1.tile([P, HIDDEN, PACK], BF16, align_bytes=64)
+                for hb in range(HIDDEN // P):
+                    h_cols = slice(P * hb, P * (hb + 1))
+                    z_ps = work.tile([P, PACK, P], F32, tag="work")
+                    for t in range(PACK):
+                        n_cols = slice(P * t, P * (t + 1))
+                        nc.tensor.matmul_mx(
+                            out=z_ps[:, t, :],
+                            lhsT=x_codes[b, g][:, n_cols].bitcast(FP8X4),
+                            lhsT_scale=x_scales[b, g][:, n_cols],
+                            rhs=w_codes[:, h_cols].bitcast(FP8X4),
+                            rhs_scale=w_scales[:, h_cols],
+                            start=True,
+                            stop=True,
+                        )
+                    copy = nc.vector.tensor_copy if hb % 2 == 0 else nc.scalar.copy
+                    copy(out=z_grouped[:, h_cols, :], in_=z_ps[:].rearrange("p t h -> p h t"))
+                nc.vector.quantize_mx(
+                    out=z_codes[b][:, g, :].bitcast(FP8X4),
+                    scales=z_scales[b][:, g, :],
+                    in_=z_grouped[:].rearrange("p h t -> p (h t)"),
+                )
+
+            groups = [(b, g) for b in range(GRAPHS) for g in range(PASSES)]
+            for n, (b, g) in enumerate(groups):
+                features_to_codes(b, g)
+                if n >= 1:
+                    project(*groups[n - 1])
+            project(*groups[-1])
+
+            bias_ps = work.tile([P, HIDDEN], F32, tag="work")
+            nc.tensor.matmul(out=bias_ps[:], lhsT=ones[:], rhs=bias_in[:], start=True, stop=True)
+            nc.vector.tensor_copy(out=bias_row[:], in_=bias_ps[:])
+
+        c_ps = {}
+        d_ps = {}
+        c = [keep.tile([P, CHUNKS], F32, name="c%d" % b) for b in range(GRAPHS)]
+        root = [keep.tile([P, CHUNKS], F32, name="root%d" % b) for b in range(GRAPHS)]
+
+        def degree_piece(b, piece):
+            if piece < 2 * PASSES:
+                g, half = divmod(piece, 2)
+                if piece == 0:
+                    c_ps[b] = work.tile([P, PASSES, CHUNKS, ONES_N], F32, tag="work", name="c_ps")
+                for m in range(HALF * half, HALF * (half + 1)):
+                    for t in range(PACK):
+                        nc.tensor.matmul(
+                            out=c_ps[b][:, g, m, :],
+                            lhsT=adj_sb[b][g][:, t, P * m : P * (m + 1)],
+                            rhs=ones[:, :ONES_N],
+                            start=(t == 0),
+                            stop=(t == PACK - 1),
+                        )
+            elif piece == 2 * PASSES:
+                nc.vector.tensor_reduce(
+                    out=c[b][:],
+                    in_=c_ps[b][:, :, :, 0].rearrange("p g m -> p m g"),
+                    axis=mybir.AxisListType.X,
+                    op=ALU.add,
+                )
+                nc.vector.tensor_scalar_max(out=root[b][:], in0=c[b][:], scalar1=1e-30)
+                nc.scalar.activation(out=root[b][:], in_=root[b][:], func=ACT.Sqrt)
+            elif piece == 2 * PASSES + 1:
+                nc.vector.reciprocal(out=root[b][:], in_=root[b][:])
+                nc.vector.scalar_tensor_tensor(
+                    out=d_col[b][:], in0=c[b][:], scalar=0.0, in1=root[b][:], op0=ALU.is_gt, op1=ALU.mult
+                )
+                for q in range(BLOCKS):
+                    d_ps[b, q] = work.tile([P, BLOCK], F32, tag="work", name="d_ps")
+                    for m in range(ROW_TILES):
+                        r = ROW_TILES * q + m
+                        nc.tensor.transpose(
+                            d_ps[b, q][:, P * m : P * (m + 1)],
+                            d_col[b][:, r : r + 1].to_broadcast([P, P]),
+                            ident[:],
+                        )
+            else:
+                for q in range(2 * (piece - 2 * PASSES - 2), 2 * (piece - 2 * PASSES - 1)):
+                    nc.scalar.copy(out=d_row[b][:, BLOCK * q : BLOCK * (q + 1)], in_=d_ps[b, q][:])
+
+        for piece in range(DEGREE_PIECES):
+            degree_piece(0, piece)
+
+        rows3 = ctx.enter_context(tc.tile_pool(name="rows3", bufs=3))
+        codes = ctx.enter_context(tc.tile_pool(name="codes", bufs=2))
+        outs = ctx.enter_context(tc.tile_pool(name="outs", bufs=2 * ROW_TILES))
+        a_grouped = {}
+        a_codes = {}
+        a_scales = {}
+        acc = {}
+
+        def scale(b, ib, g):
+            i_cols = slice(BLOCK * ib, BLOCK * (ib + 1))
+            a_planes = rows3.tile([P, PACK, BLOCK], BF16)
+            for t in range(PACK):
+                r = PACK * g + t
+                nc.vector.scalar_tensor_tensor(
+                    out=a_planes[:, t, :],
+                    in0=adj_sb[b][g][:, t, i_cols],
+                    scalar=d_col[b][:, r : r + 1],
+                    in1=d_row[b][:, i_cols],
+                    op0=ALU.mult,
+                    op1=ALU.mult,
+                )
+            a_grouped[b, ib, g] = rows3.tile([P, BLOCK, PACK], BF16, align_bytes=64, name="a_grouped")
+            side_by_side(nc.scalar.copy, a_grouped[b, ib, g][:], a_planes[:])
+
+        def quantise_and_multiply(b, ib, g):
+            if g == 0:
+                a_codes[b, ib] = codes.tile([P, PASSES, BLOCK], U32, align_bytes=64, name="a_codes")
+                a_scales[b, ib] = codes.tile([P, PASSES, BLOCK], U8, align_bytes=64, name="a_scales")
+                acc[b, ib] = [
+                    sums.tile([P, HIDDEN], F32, name="acc%d" % m, tag="acc") for m in range(ROW_TILES)
+                ]
+            nc.vector.quantize_mx(
+                out=a_codes[b, ib][:, g, :].bitcast(FP8X4),
+                scales=a_scales[b, ib][:, g, :],
+                in_=a_grouped[b, ib, g][:].rearrange("p i t -> p (i t)"),
+            )
+            for m in range(ROW_TILES):
+                m_cols = slice(P * m, P * (m + 1))
+                nc.tensor.matmul_mx(
+                    out=acc[b, ib][m][:],
+                    lhsT=a_codes[b, ib][:, g, m_cols].bitcast(FP8X4),
+                    lhsT_scale=a_scales[b, ib][:, g, m_cols],
+                    rhs=z_codes[b][:, g, :].bitcast(FP8X4),
+                    rhs_scale=z_scales[b][:, g, :],
+                    start=(g == 0),
+                    stop=(g == PASSES - 1),
+                )
+
+        def finish(b, ib):
+            for m in range(ROW_TILES):
+                y = outs.tile([P, HIDDEN], F32)
+                nc.vector.tensor_tensor(out=y[:], in0=acc[b, ib][m][:], in1=bias_row[:], op=ALU.add)
+                nc.scalar.activation(out=y[:], in_=y[:], func=ACT.Relu)
+                row0 = BLOCK * ib + P * m
+                nc.sync.dma_start(out=out[b, row0 : row0 + P, :], in_=y[:])
+
+        steps = [(b, ib, g) for b in range(GRAPHS) for ib in range(BLOCKS) for g in range(PASSES)]
+        for n, (b, ib, g) in enumerate(steps):
+            scale(b, ib, g)
+            if n >= 2 and steps[n - 2][2] == PASSES - 1:
+                finish(*steps[n - 2][:2])
+            if n >= 1:
+                quantise_and_multiply(*steps[n - 1])
+            piece = n % STEPS - (STEPS - DEGREE_PIECES)
+            if b + 1 < GRAPHS and piece >= 0:
+                degree_piece(b + 1, piece)
+        quantise_and_multiply(*steps[-1])
+        finish(*steps[-1][:2])

@@ -22,9 +22,10 @@ BLOCK = 512
 BLOCKS = NODES // BLOCK
 ROW_TILES = BLOCK // P
 ONES_N = 8
-STEPS = BLOCKS * PASSES
-HALF = CHUNKS // 2
-DEGREE_PIECES = 2 * PASSES + 4
+HALF = NODES // 2
+HALF_CHUNKS = CHUNKS // 2
+EARLY = 2
+DEGREE_PIECES = 5
 
 FLOPS = 2 * GRAPHS * NODES * FEATS * HIDDEN + 2 * GRAPHS * NODES * NODES * HIDDEN
 
@@ -52,10 +53,12 @@ def tile_perception_pa_kernel(tc, batch_graph, adj, W1, b1, out):
         nc.vector.memset(warm[:], 1.0)
         nc.scalar.activation(out=warm[:], in_=warm[:], func=ACT.Sqrt)
 
-        adj_sb = [
-            [keep.tile([P, PACK, NODES], BF16, name="adj%d_%d" % (b, g)) for g in range(PASSES)]
+        adj_sb = {
+            (b, h, v): keep.tile([P, HALF_CHUNKS, HALF], BF16, name="adj%d_%d%d" % (b, h, v))
             for b in range(GRAPHS)
-        ]
+            for h in range(2)
+            for v in range(2)
+        }
         z_codes = [
             keep.tile([P, PASSES, HIDDEN], U32, align_bytes=64, name="z_codes%d" % b)
             for b in range(GRAPHS)
@@ -89,8 +92,14 @@ def tile_perception_pa_kernel(tc, batch_graph, adj, W1, b1, out):
             nc.sync.dma_start(out=bias_in[0:1, :], in_=b1.rearrange("(o h) -> o h", o=1))
             for b in range(GRAPHS):
                 adj_chunks = adj[b].rearrange("(r p) i -> p r i", p=P)
-                for g in range(PASSES):
-                    nc.sync.dma_start(out=adj_sb[b][g][:], in_=adj_chunks[:, PACK * g : PACK * (g + 1), :])
+                for h in range(2):
+                    for v in range(2):
+                        nc.sync.dma_start(
+                            out=adj_sb[b, h, v][:],
+                            in_=adj_chunks[
+                                :, HALF_CHUNKS * v : HALF_CHUNKS * (v + 1), HALF * h : HALF * (h + 1)
+                            ],
+                        )
 
             w_grouped = feats.tile([P, HIDDEN, PACK], BF16, align_bytes=64)
             side_by_side(nc.vector.tensor_copy, w_grouped[:], w_planes[:])
@@ -172,35 +181,41 @@ def tile_perception_pa_kernel(tc, batch_graph, adj, W1, b1, out):
         c = [keep.tile([P, CHUNKS], F32, name="c%d" % b) for b in range(GRAPHS)]
         root = [keep.tile([P, CHUNKS], F32, name="root%d" % b) for b in range(GRAPHS)]
 
-        def degree_piece(b, piece):
-            if piece < 2 * PASSES:
-                g, half = divmod(piece, 2)
-                if piece == 0:
-                    c_ps[b] = work.tile([P, PASSES, CHUNKS, ONES_N], F32, tag="work", name="c_ps")
-                for m in range(HALF * half, HALF * (half + 1)):
-                    for t in range(PACK):
+        def degree_piece(b, h, piece):
+            chunks = slice(HALF_CHUNKS * h, HALF_CHUNKS * (h + 1))
+            if piece < 2:
+                v = piece
+                if v == 0:
+                    c_ps[b, h] = work.tile([P, 2, HALF_CHUNKS, ONES_N], F32, tag="work", name="c_ps")
+                for m in range(HALF_CHUNKS):
+                    for r in range(HALF_CHUNKS):
                         nc.tensor.matmul(
-                            out=c_ps[b][:, g, m, :],
-                            lhsT=adj_sb[b][g][:, t, P * m : P * (m + 1)],
+                            out=c_ps[b, h][:, v, m, :],
+                            lhsT=adj_sb[b, h, v][:, r, P * m : P * (m + 1)],
                             rhs=ones[:, :ONES_N],
-                            start=(t == 0),
-                            stop=(t == PACK - 1),
+                            start=(r == 0),
+                            stop=(r == HALF_CHUNKS - 1),
                         )
-            elif piece == 2 * PASSES:
+            elif piece == 2:
                 nc.vector.tensor_reduce(
-                    out=c[b][:],
-                    in_=c_ps[b][:, :, :, 0].rearrange("p g m -> p m g"),
+                    out=c[b][:, chunks],
+                    in_=c_ps[b, h][:, :, :, 0].rearrange("p v m -> p m v"),
                     axis=mybir.AxisListType.X,
                     op=ALU.add,
                 )
-                nc.vector.tensor_scalar_max(out=root[b][:], in0=c[b][:], scalar1=1e-30)
-                nc.scalar.activation(out=root[b][:], in_=root[b][:], func=ACT.Sqrt)
-            elif piece == 2 * PASSES + 1:
-                nc.vector.reciprocal(out=root[b][:], in_=root[b][:])
+                nc.vector.tensor_scalar_max(out=root[b][:, chunks], in0=c[b][:, chunks], scalar1=1e-30)
+                nc.scalar.activation(out=root[b][:, chunks], in_=root[b][:, chunks], func=ACT.Sqrt)
+            elif piece == 3:
+                nc.vector.reciprocal(out=root[b][:, chunks], in_=root[b][:, chunks])
                 nc.vector.scalar_tensor_tensor(
-                    out=d_col[b][:], in0=c[b][:], scalar=0.0, in1=root[b][:], op0=ALU.is_gt, op1=ALU.mult
+                    out=d_col[b][:, chunks],
+                    in0=c[b][:, chunks],
+                    scalar=0.0,
+                    in1=root[b][:, chunks],
+                    op0=ALU.is_gt,
+                    op1=ALU.mult,
                 )
-                for q in range(BLOCKS):
+                for q in range(EARLY * h, EARLY * (h + 1)):
                     d_ps[b, q] = work.tile([P, BLOCK], F32, tag="work", name="d_ps")
                     for m in range(ROW_TILES):
                         r = ROW_TILES * q + m
@@ -210,11 +225,15 @@ def tile_perception_pa_kernel(tc, batch_graph, adj, W1, b1, out):
                             ident[:],
                         )
             else:
-                for q in range(2 * (piece - 2 * PASSES - 2), 2 * (piece - 2 * PASSES - 1)):
+                for q in range(EARLY * h, EARLY * (h + 1)):
                     nc.scalar.copy(out=d_row[b][:, BLOCK * q : BLOCK * (q + 1)], in_=d_ps[b, q][:])
 
-        for piece in range(DEGREE_PIECES):
-            degree_piece(0, piece)
+        pieces = [
+            (b, h, piece) for b in range(GRAPHS) for h in range(2) for piece in range(DEGREE_PIECES)
+        ]
+        for piece in pieces[:DEGREE_PIECES]:
+            degree_piece(*piece)
+        background = pieces[DEGREE_PIECES:]
 
         rows3 = ctx.enter_context(tc.tile_pool(name="rows3", bufs=3))
         codes = ctx.enter_context(tc.tile_pool(name="codes", bufs=2))
@@ -226,12 +245,13 @@ def tile_perception_pa_kernel(tc, batch_graph, adj, W1, b1, out):
 
         def scale(b, ib, g):
             i_cols = slice(BLOCK * ib, BLOCK * (ib + 1))
+            h_cols = slice(BLOCK * (ib % EARLY), BLOCK * (ib % EARLY + 1))
             a_planes = rows3.tile([P, PACK, BLOCK], BF16)
             for t in range(PACK):
                 r = PACK * g + t
                 nc.vector.scalar_tensor_tensor(
                     out=a_planes[:, t, :],
-                    in0=adj_sb[b][g][:, t, i_cols],
+                    in0=adj_sb[b, ib // EARLY, g // EARLY][:, r % HALF_CHUNKS, h_cols],
                     scalar=d_col[b][:, r : r + 1],
                     in1=d_row[b][:, i_cols],
                     op0=ALU.mult,
@@ -244,25 +264,30 @@ def tile_perception_pa_kernel(tc, batch_graph, adj, W1, b1, out):
             if g == 0:
                 a_codes[b, ib] = codes.tile([P, PASSES, BLOCK], U32, align_bytes=64, name="a_codes")
                 a_scales[b, ib] = codes.tile([P, PASSES, BLOCK], U8, align_bytes=64, name="a_scales")
-                acc[b, ib] = [
-                    sums.tile([P, HIDDEN], F32, name="acc%d" % m, tag="acc") for m in range(ROW_TILES)
-                ]
             nc.vector.quantize_mx(
                 out=a_codes[b, ib][:, g, :].bitcast(FP8X4),
                 scales=a_scales[b, ib][:, g, :],
                 in_=a_grouped[b, ib, g][:].rearrange("p i t -> p (i t)"),
             )
-            for m in range(ROW_TILES):
-                m_cols = slice(P * m, P * (m + 1))
-                nc.tensor.matmul_mx(
-                    out=acc[b, ib][m][:],
-                    lhsT=a_codes[b, ib][:, g, m_cols].bitcast(FP8X4),
-                    lhsT_scale=a_scales[b, ib][:, g, m_cols],
-                    rhs=z_codes[b][:, g, :].bitcast(FP8X4),
-                    rhs_scale=z_scales[b][:, g, :],
-                    start=(g == 0),
-                    stop=(g == PASSES - 1),
-                )
+            held = 0 < ib < EARLY
+            if held and g < EARLY:
+                return
+            for gg in range(0 if held and g == EARLY else g, g + 1):
+                if gg == 0:
+                    acc[b, ib] = [
+                        sums.tile([P, HIDDEN], F32, name="acc%d" % m, tag="acc") for m in range(ROW_TILES)
+                    ]
+                for m in range(ROW_TILES):
+                    m_cols = slice(P * m, P * (m + 1))
+                    nc.tensor.matmul_mx(
+                        out=acc[b, ib][m][:],
+                        lhsT=a_codes[b, ib][:, gg, m_cols].bitcast(FP8X4),
+                        lhsT_scale=a_scales[b, ib][:, gg, m_cols],
+                        rhs=z_codes[b][:, gg, :].bitcast(FP8X4),
+                        rhs_scale=z_scales[b][:, gg, :],
+                        start=(gg == 0),
+                        stop=(gg == PASSES - 1),
+                    )
 
         def finish(b, ib):
             for m in range(ROW_TILES):
@@ -272,15 +297,17 @@ def tile_perception_pa_kernel(tc, batch_graph, adj, W1, b1, out):
                 row0 = BLOCK * ib + P * m
                 nc.sync.dma_start(out=out[b, row0 : row0 + P, :], in_=y[:])
 
-        steps = [(b, ib, g) for b in range(GRAPHS) for ib in range(BLOCKS) for g in range(PASSES)]
-        for n, (b, ib, g) in enumerate(steps):
-            scale(b, ib, g)
+        pairs = [(ib, g) for ib in range(BLOCKS) for g in range(PASSES)]
+        early = [(ib, g) for ib, g in pairs if ib < EARLY and g < EARLY]
+        late = [(ib, g) for ib, g in pairs if not (ib < EARLY and g < EARLY)]
+        steps = [(b, ib, g) for b in range(GRAPHS) for ib, g in early + late]
+        for n, step in enumerate(steps):
+            scale(*step)
             if n >= 2 and steps[n - 2][2] == PASSES - 1:
                 finish(*steps[n - 2][:2])
             if n >= 1:
                 quantise_and_multiply(*steps[n - 1])
-            piece = n % STEPS - (STEPS - DEGREE_PIECES)
-            if b + 1 < GRAPHS and piece >= 0:
-                degree_piece(b + 1, piece)
+            if n < len(background):
+                degree_piece(*background[n])
         quantise_and_multiply(*steps[-1])
         finish(*steps[-1][:2])

@@ -22,10 +22,9 @@ BLOCK = 512
 BLOCKS = NODES // BLOCK
 ROW_TILES = BLOCK // P
 ONES_N = 8
-HALF = NODES // 2
-HALF_CHUNKS = CHUNKS // 2
-EARLY = 2
-DEGREE_PIECES = 5
+STEPS = BLOCKS * PASSES
+HALF = CHUNKS // 2
+DEGREE_PIECES = 2 * PASSES + 4
 
 FLOPS = 2 * GRAPHS * NODES * FEATS * HIDDEN + 2 * GRAPHS * NODES * NODES * HIDDEN
 
@@ -40,7 +39,6 @@ def side_by_side(copy, grouped, planes):
 def tile_perception_pa_kernel(tc, batch_graph, adj, W1, b1, out):
     nc = tc.nc
     with ExitStack() as ctx:
-        ctx.enter_context(tc.manual_schedule())
         keep = ctx.enter_context(tc.tile_pool(name="keep", bufs=1))
         work = ctx.enter_context(tc.psum_pool(name="work", bufs=4))
         sums = ctx.enter_context(tc.psum_pool(name="sums", bufs=ROW_TILES))
@@ -53,12 +51,10 @@ def tile_perception_pa_kernel(tc, batch_graph, adj, W1, b1, out):
         nc.vector.memset(warm[:], 1.0)
         nc.scalar.activation(out=warm[:], in_=warm[:], func=ACT.Sqrt)
 
-        adj_sb = {
-            (b, h, v): keep.tile([P, HALF_CHUNKS, HALF], BF16, name="adj%d_%d%d" % (b, h, v))
+        adj_sb = [
+            [keep.tile([P, PACK, NODES], BF16, name="adj%d_%d" % (b, g)) for g in range(PASSES)]
             for b in range(GRAPHS)
-            for h in range(2)
-            for v in range(2)
-        }
+        ]
         z_codes = [
             keep.tile([P, PASSES, HIDDEN], U32, align_bytes=64, name="z_codes%d" % b)
             for b in range(GRAPHS)
@@ -92,14 +88,8 @@ def tile_perception_pa_kernel(tc, batch_graph, adj, W1, b1, out):
             nc.sync.dma_start(out=bias_in[0:1, :], in_=b1.rearrange("(o h) -> o h", o=1))
             for b in range(GRAPHS):
                 adj_chunks = adj[b].rearrange("(r p) i -> p r i", p=P)
-                for h in range(2):
-                    for v in range(2):
-                        nc.sync.dma_start(
-                            out=adj_sb[b, h, v][:],
-                            in_=adj_chunks[
-                                :, HALF_CHUNKS * v : HALF_CHUNKS * (v + 1), HALF * h : HALF * (h + 1)
-                            ],
-                        )
+                for g in range(PASSES):
+                    nc.sync.dma_start(out=adj_sb[b][g][:], in_=adj_chunks[:, PACK * g : PACK * (g + 1), :])
 
             w_grouped = feats.tile([P, HIDDEN, PACK], BF16, align_bytes=64)
             side_by_side(nc.vector.tensor_copy, w_grouped[:], w_planes[:])
@@ -181,41 +171,35 @@ def tile_perception_pa_kernel(tc, batch_graph, adj, W1, b1, out):
         c = [keep.tile([P, CHUNKS], F32, name="c%d" % b) for b in range(GRAPHS)]
         root = [keep.tile([P, CHUNKS], F32, name="root%d" % b) for b in range(GRAPHS)]
 
-        def degree_piece(b, h, piece):
-            chunks = slice(HALF_CHUNKS * h, HALF_CHUNKS * (h + 1))
-            if piece < 2:
-                v = piece
-                if v == 0:
-                    c_ps[b, h] = work.tile([P, 2, HALF_CHUNKS, ONES_N], F32, tag="work", name="c_ps")
-                for m in range(HALF_CHUNKS):
-                    for r in range(HALF_CHUNKS):
+        def degree_piece(b, piece):
+            if piece < 2 * PASSES:
+                g, half = divmod(piece, 2)
+                if piece == 0:
+                    c_ps[b] = work.tile([P, PASSES, CHUNKS, ONES_N], F32, tag="work", name="c_ps")
+                for m in range(HALF * half, HALF * (half + 1)):
+                    for t in range(PACK):
                         nc.tensor.matmul(
-                            out=c_ps[b, h][:, v, m, :],
-                            lhsT=adj_sb[b, h, v][:, r, P * m : P * (m + 1)],
+                            out=c_ps[b][:, g, m, :],
+                            lhsT=adj_sb[b][g][:, t, P * m : P * (m + 1)],
                             rhs=ones[:, :ONES_N],
-                            start=(r == 0),
-                            stop=(r == HALF_CHUNKS - 1),
+                            start=(t == 0),
+                            stop=(t == PACK - 1),
                         )
-            elif piece == 2:
+            elif piece == 2 * PASSES:
                 nc.vector.tensor_reduce(
-                    out=c[b][:, chunks],
-                    in_=c_ps[b, h][:, :, :, 0].rearrange("p v m -> p m v"),
+                    out=c[b][:],
+                    in_=c_ps[b][:, :, :, 0].rearrange("p g m -> p m g"),
                     axis=mybir.AxisListType.X,
                     op=ALU.add,
                 )
-                nc.vector.tensor_scalar_max(out=root[b][:, chunks], in0=c[b][:, chunks], scalar1=1e-30)
-                nc.scalar.activation(out=root[b][:, chunks], in_=root[b][:, chunks], func=ACT.Sqrt)
-            elif piece == 3:
-                nc.vector.reciprocal(out=root[b][:, chunks], in_=root[b][:, chunks])
+                nc.vector.tensor_scalar_max(out=root[b][:], in0=c[b][:], scalar1=1e-30)
+                nc.scalar.activation(out=root[b][:], in_=root[b][:], func=ACT.Sqrt)
+            elif piece == 2 * PASSES + 1:
+                nc.vector.reciprocal(out=root[b][:], in_=root[b][:])
                 nc.vector.scalar_tensor_tensor(
-                    out=d_col[b][:, chunks],
-                    in0=c[b][:, chunks],
-                    scalar=0.0,
-                    in1=root[b][:, chunks],
-                    op0=ALU.is_gt,
-                    op1=ALU.mult,
+                    out=d_col[b][:], in0=c[b][:], scalar=0.0, in1=root[b][:], op0=ALU.is_gt, op1=ALU.mult
                 )
-                for q in range(EARLY * h, EARLY * (h + 1)):
+                for q in range(BLOCKS):
                     d_ps[b, q] = work.tile([P, BLOCK], F32, tag="work", name="d_ps")
                     for m in range(ROW_TILES):
                         r = ROW_TILES * q + m
@@ -225,15 +209,11 @@ def tile_perception_pa_kernel(tc, batch_graph, adj, W1, b1, out):
                             ident[:],
                         )
             else:
-                for q in range(EARLY * h, EARLY * (h + 1)):
+                for q in range(2 * (piece - 2 * PASSES - 2), 2 * (piece - 2 * PASSES - 1)):
                     nc.scalar.copy(out=d_row[b][:, BLOCK * q : BLOCK * (q + 1)], in_=d_ps[b, q][:])
 
-        pieces = [
-            (b, h, piece) for b in range(GRAPHS) for h in range(2) for piece in range(DEGREE_PIECES)
-        ]
-        for piece in pieces[:DEGREE_PIECES]:
-            degree_piece(*piece)
-        background = pieces[DEGREE_PIECES:]
+        for piece in range(DEGREE_PIECES):
+            degree_piece(0, piece)
 
         rows3 = ctx.enter_context(tc.tile_pool(name="rows3", bufs=3))
         codes = ctx.enter_context(tc.tile_pool(name="codes", bufs=2))
@@ -245,13 +225,12 @@ def tile_perception_pa_kernel(tc, batch_graph, adj, W1, b1, out):
 
         def scale(b, ib, g):
             i_cols = slice(BLOCK * ib, BLOCK * (ib + 1))
-            h_cols = slice(BLOCK * (ib % EARLY), BLOCK * (ib % EARLY + 1))
             a_planes = rows3.tile([P, PACK, BLOCK], BF16)
             for t in range(PACK):
                 r = PACK * g + t
                 nc.vector.scalar_tensor_tensor(
                     out=a_planes[:, t, :],
-                    in0=adj_sb[b, ib // EARLY, g // EARLY][:, r % HALF_CHUNKS, h_cols],
+                    in0=adj_sb[b][g][:, t, i_cols],
                     scalar=d_col[b][:, r : r + 1],
                     in1=d_row[b][:, i_cols],
                     op0=ALU.mult,
@@ -264,30 +243,25 @@ def tile_perception_pa_kernel(tc, batch_graph, adj, W1, b1, out):
             if g == 0:
                 a_codes[b, ib] = codes.tile([P, PASSES, BLOCK], U32, align_bytes=64, name="a_codes")
                 a_scales[b, ib] = codes.tile([P, PASSES, BLOCK], U8, align_bytes=64, name="a_scales")
+                acc[b, ib] = [
+                    sums.tile([P, HIDDEN], F32, name="acc%d" % m, tag="acc") for m in range(ROW_TILES)
+                ]
             nc.vector.quantize_mx(
                 out=a_codes[b, ib][:, g, :].bitcast(FP8X4),
                 scales=a_scales[b, ib][:, g, :],
                 in_=a_grouped[b, ib, g][:].rearrange("p i t -> p (i t)"),
             )
-            held = 0 < ib < EARLY
-            if held and g < EARLY:
-                return
-            for gg in range(0 if held and g == EARLY else g, g + 1):
-                if gg == 0:
-                    acc[b, ib] = [
-                        sums.tile([P, HIDDEN], F32, name="acc%d" % m, tag="acc") for m in range(ROW_TILES)
-                    ]
-                for m in range(ROW_TILES):
-                    m_cols = slice(P * m, P * (m + 1))
-                    nc.tensor.matmul_mx(
-                        out=acc[b, ib][m][:],
-                        lhsT=a_codes[b, ib][:, gg, m_cols].bitcast(FP8X4),
-                        lhsT_scale=a_scales[b, ib][:, gg, m_cols],
-                        rhs=z_codes[b][:, gg, :].bitcast(FP8X4),
-                        rhs_scale=z_scales[b][:, gg, :],
-                        start=(gg == 0),
-                        stop=(gg == PASSES - 1),
-                    )
+            for m in range(ROW_TILES):
+                m_cols = slice(P * m, P * (m + 1))
+                nc.tensor.matmul_mx(
+                    out=acc[b, ib][m][:],
+                    lhsT=a_codes[b, ib][:, g, m_cols].bitcast(FP8X4),
+                    lhsT_scale=a_scales[b, ib][:, g, m_cols],
+                    rhs=z_codes[b][:, g, :].bitcast(FP8X4),
+                    rhs_scale=z_scales[b][:, g, :],
+                    start=(g == 0),
+                    stop=(g == PASSES - 1),
+                )
 
         def finish(b, ib):
             for m in range(ROW_TILES):
@@ -297,17 +271,15 @@ def tile_perception_pa_kernel(tc, batch_graph, adj, W1, b1, out):
                 row0 = BLOCK * ib + P * m
                 nc.sync.dma_start(out=out[b, row0 : row0 + P, :], in_=y[:])
 
-        pairs = [(ib, g) for ib in range(BLOCKS) for g in range(PASSES)]
-        early = [(ib, g) for ib, g in pairs if ib < EARLY and g < EARLY]
-        late = [(ib, g) for ib, g in pairs if not (ib < EARLY and g < EARLY)]
-        steps = [(b, ib, g) for b in range(GRAPHS) for ib, g in early + late]
-        for n, step in enumerate(steps):
-            scale(*step)
+        steps = [(b, ib, g) for b in range(GRAPHS) for ib in range(BLOCKS) for g in range(PASSES)]
+        for n, (b, ib, g) in enumerate(steps):
+            scale(b, ib, g)
             if n >= 2 and steps[n - 2][2] == PASSES - 1:
                 finish(*steps[n - 2][:2])
             if n >= 1:
                 quantise_and_multiply(*steps[n - 1])
-            if n < len(background):
-                degree_piece(*background[n])
+            piece = n % STEPS - (STEPS - DEGREE_PIECES)
+            if b + 1 < GRAPHS and piece >= 0:
+                degree_piece(b + 1, piece)
         quantise_and_multiply(*steps[-1])
         finish(*steps[-1][:2])

@@ -21,10 +21,12 @@ PASSES = NODES // K_PASS
 BLOCK = 512
 BLOCKS = NODES // BLOCK
 ROW_TILES = BLOCK // P
-ONES_N = 8
 STEPS = BLOCKS * PASSES
 HALF = CHUNKS // 2
-DEGREE_PIECES = 2 * PASSES + 4
+SUM_PIECES = 2 * PASSES
+DEGREE_PIECES = SUM_PIECES + 6
+PARTS = 3
+TERMS = PARTS * PARTS
 
 FLOPS = 2 * GRAPHS * NODES * FEATS * HIDDEN + 2 * GRAPHS * NODES * NODES * HIDDEN
 
@@ -40,11 +42,12 @@ def tile_perception_pa_kernel(tc, batch_graph, adj, W1, b1, out):
     nc = tc.nc
     with ExitStack() as ctx:
         keep = ctx.enter_context(tc.tile_pool(name="keep", bufs=1))
-        work = ctx.enter_context(tc.psum_pool(name="work", bufs=4))
-        sums = ctx.enter_context(tc.psum_pool(name="sums", bufs=ROW_TILES))
+        degrees = ctx.enter_context(tc.psum_pool(name="degrees", bufs=1))
 
         ident = keep.tile([P, P], F32)
         make_identity(nc, ident[:])
+        ident_bf = keep.tile([P, P], BF16)
+        make_identity(nc, ident_bf[:])
         ones = keep.tile([P, P], BF16)
         nc.vector.memset(ones[:], 1.0)
         warm = keep.tile([P, 1], F32)
@@ -64,12 +67,12 @@ def tile_perception_pa_kernel(tc, batch_graph, adj, W1, b1, out):
             for b in range(GRAPHS)
         ]
         d_col = [keep.tile([P, CHUNKS], F32, name="d_col%d" % b) for b in range(GRAPHS)]
-        d_row = [keep.tile([P, NODES], F32, name="d_row%d" % b) for b in range(GRAPHS)]
         bias_row = keep.tile([P, HIDDEN], F32)
 
         with ExitStack() as stage1:
             feats = stage1.enter_context(tc.tile_pool(name="feats", bufs=1))
             rows1 = stage1.enter_context(tc.tile_pool(name="rows1", bufs=2))
+            work = stage1.enter_context(tc.psum_pool(name="work", bufs=7))
 
             w_planes = feats.tile([P, PACK, HIDDEN], BF16)
             for u in range(2):
@@ -166,67 +169,153 @@ def tile_perception_pa_kernel(tc, batch_graph, adj, W1, b1, out):
             nc.tensor.matmul(out=bias_ps[:], lhsT=ones[:], rhs=bias_in[:], start=True, stop=True)
             nc.vector.tensor_copy(out=bias_row[:], in_=bias_ps[:])
 
+        late = ctx.enter_context(tc.tile_pool(name="late", bufs=1))
+        d_row = {}
+        d_left = [late.tile([P, NODES], BF16, name="d_left%d" % b) for b in range(GRAPHS)]
+        d_right = [late.tile([P, NODES], BF16, name="d_right%d" % b) for b in range(GRAPHS)]
+        left_cols = late.tile([P, CHUNKS, P], BF16)
+        right_cols = late.tile([P, CHUNKS, P], BF16)
+        nc.gpsimd.memset(left_cols[:], 0.0)
+        nc.gpsimd.memset(right_cols[:], 0.0)
+        sums = ctx.enter_context(tc.psum_pool(name="sums", bufs=ROW_TILES))
+        spread = ctx.enter_context(tc.psum_pool(name="spread", bufs=3))
         c_ps = {}
-        d_ps = {}
         c = [keep.tile([P, CHUNKS], F32, name="c%d" % b) for b in range(GRAPHS)]
         root = [keep.tile([P, CHUNKS], F32, name="root%d" % b) for b in range(GRAPHS)]
+        rest = [keep.tile([P, CHUNKS], F32, name="rest%d" % b) for b in range(GRAPHS)]
+        parts = [keep.tile([P, CHUNKS, PARTS], BF16, name="parts%d" % b) for b in range(GRAPHS)]
 
         def degree_piece(b, piece):
-            if piece < 2 * PASSES:
+            if piece < SUM_PIECES:
                 g, half = divmod(piece, 2)
                 if piece == 0:
-                    c_ps[b] = work.tile([P, PASSES, CHUNKS, ONES_N], F32, tag="work", name="c_ps")
+                    c_ps[b] = degrees.tile([P, PASSES, CHUNKS], F32, tag="degrees", name="c_ps")
                 for m in range(HALF * half, HALF * (half + 1)):
                     for t in range(PACK):
                         nc.tensor.matmul(
-                            out=c_ps[b][:, g, m, :],
+                            out=c_ps[b][:, g, m : m + 1],
                             lhsT=adj_sb[b][g][:, t, P * m : P * (m + 1)],
-                            rhs=ones[:, :ONES_N],
+                            rhs=ones[:, 0:1],
                             start=(t == 0),
                             stop=(t == PACK - 1),
                         )
-            elif piece == 2 * PASSES:
+            elif piece == SUM_PIECES:
                 nc.vector.tensor_reduce(
                     out=c[b][:],
-                    in_=c_ps[b][:, :, :, 0].rearrange("p g m -> p m g"),
+                    in_=c_ps[b][:].rearrange("p g m -> p m g"),
                     axis=mybir.AxisListType.X,
                     op=ALU.add,
                 )
                 nc.vector.tensor_scalar_max(out=root[b][:], in0=c[b][:], scalar1=1e-30)
                 nc.scalar.activation(out=root[b][:], in_=root[b][:], func=ACT.Sqrt)
-            elif piece == 2 * PASSES + 1:
+            elif piece == SUM_PIECES + 1:
                 nc.vector.reciprocal(out=root[b][:], in_=root[b][:])
                 nc.vector.scalar_tensor_tensor(
                     out=d_col[b][:], in0=c[b][:], scalar=0.0, in1=root[b][:], op0=ALU.is_gt, op1=ALU.mult
                 )
-                for q in range(BLOCKS):
-                    d_ps[b, q] = work.tile([P, BLOCK], F32, tag="work", name="d_ps")
+                nc.vector.tensor_copy(out=parts[b][:, :, 0], in_=d_col[b][:])
+                nc.vector.tensor_sub(out=rest[b][:], in0=d_col[b][:], in1=parts[b][:, :, 0])
+                nc.vector.tensor_copy(out=parts[b][:, :, 1], in_=rest[b][:])
+                nc.vector.tensor_sub(out=rest[b][:], in0=rest[b][:], in1=parts[b][:, :, 1])
+                nc.vector.tensor_copy(out=parts[b][:, :, 2], in_=rest[b][:])
+                nc.vector.tensor_copy(
+                    out=left_cols[:, :, :TERMS].rearrange("p r (u v) -> p r u v", v=PARTS),
+                    in_=parts[b][:].unsqueeze(3).to_broadcast([P, CHUNKS, PARTS, PARTS]),
+                )
+                nc.vector.tensor_copy(
+                    out=right_cols[:, :, :TERMS].rearrange("p r (u v) -> p r u v", v=PARTS),
+                    in_=parts[b][:].unsqueeze(2).to_broadcast([P, CHUNKS, PARTS, PARTS]),
+                )
+            elif piece < SUM_PIECES + 4:
+                cols, rows = ((left_cols, d_left[b]), (right_cols, d_right[b]))[piece - SUM_PIECES - 2]
+                for h in range(2):
+                    bank = spread.tile([P, HALF, P], BF16, tag="spread", name="bank")
+                    for m in range(HALF):
+                        nc.tensor.transpose(bank[:, m, :], cols[:, HALF * h + m, :], ident_bf[:])
+                    nc.scalar.copy(
+                        out=rows[:, P * HALF * h : P * HALF * (h + 1)], in_=bank[:].rearrange("p m n -> p (m n)")
+                    )
+            else:
+                if piece == SUM_PIECES + 4:
+                    d_row[b] = late.tile([P, NODES], F32, name="d_row")
+                for q in range(2 * (piece - SUM_PIECES - 4), 2 * (piece - SUM_PIECES - 3)):
+                    d_ps = spread.tile([P, BLOCK], F32, tag="spread", name="d_ps")
                     for m in range(ROW_TILES):
                         r = ROW_TILES * q + m
                         nc.tensor.transpose(
-                            d_ps[b, q][:, P * m : P * (m + 1)],
+                            d_ps[:, P * m : P * (m + 1)],
                             d_col[b][:, r : r + 1].to_broadcast([P, P]),
                             ident[:],
                         )
-            else:
-                for q in range(2 * (piece - 2 * PASSES - 2), 2 * (piece - 2 * PASSES - 1)):
-                    nc.scalar.copy(out=d_row[b][:, BLOCK * q : BLOCK * (q + 1)], in_=d_ps[b, q][:])
+                    nc.scalar.copy(out=d_row[b][:, BLOCK * q : BLOCK * (q + 1)], in_=d_ps[:])
 
         for piece in range(DEGREE_PIECES):
             degree_piece(0, piece)
 
+        planes3 = ctx.enter_context(tc.tile_pool(name="planes3", bufs=2))
         rows3 = ctx.enter_context(tc.tile_pool(name="rows3", bufs=3))
-        codes = ctx.enter_context(tc.tile_pool(name="codes", bufs=2))
-        outs = ctx.enter_context(tc.tile_pool(name="outs", bufs=2 * ROW_TILES))
+        factors = ctx.enter_context(tc.tile_pool(name="factors", bufs=3))
+        codes = ctx.enter_context(tc.tile_pool(name="codes", bufs=3))
+        outs = ctx.enter_context(tc.tile_pool(name="outs", bufs=6))
         a_grouped = {}
-        a_codes = {}
-        a_scales = {}
         acc = {}
+        dd = {}
+
+        mirrored = ((0, 1), (0, 2), (1, 2), (2, 3))
+
+        def make_factors(b, ib, g):
+            i_cols = slice(BLOCK * ib, BLOCK * (ib + 1))
+            if (ib, g) in mirrored:
+                dd[b, ib, g] = factors.tile([P, PACK, BLOCK], BF16, name="dd_sb")
+                for t in range(PACK):
+                    r = PACK * g + t
+                    nc.vector.tensor_scalar_mul(
+                        out=dd[b, ib, g][:, t, :], in0=d_row[b][:, i_cols], scalar1=d_col[b][:, r : r + 1]
+                    )
+            elif (g, ib) in mirrored:
+                for half in range(2):
+                    dd[b, ib, g, half] = spread.tile([P, 2, BLOCK], BF16, tag="spread", name="dd")
+                    for e in range(2):
+                        t = 2 * half + e
+                        for m in range(ROW_TILES):
+                            nc.tensor.transpose(
+                                dd[b, ib, g, half][:, e, P * m : P * (m + 1)],
+                                dd[b, g, ib][:, m, P * t : P * (t + 1)],
+                                ident_bf[:],
+                            )
+            elif not by_row(b, ib, g):
+                for half in range(2):
+                    dd[b, ib, g, half] = spread.tile([P, 2, BLOCK], BF16, tag="spread", name="dd")
+                    for e in range(2):
+                        r = PACK * g + 2 * half + e
+                        nc.tensor.matmul(
+                            out=dd[b, ib, g, half][:, e, :],
+                            lhsT=d_left[b][:, P * r : P * (r + 1)],
+                            rhs=d_right[b][:, i_cols],
+                            start=True,
+                            stop=True,
+                        )
+
+        def by_row(b, ib, g):
+            return b == GRAPHS - 1 and ib == g == BLOCKS - 1
 
         def scale(b, ib, g):
             i_cols = slice(BLOCK * ib, BLOCK * (ib + 1))
-            a_planes = rows3.tile([P, PACK, BLOCK], BF16)
-            for t in range(PACK):
+            a_planes = planes3.tile([P, PACK, BLOCK], BF16)
+            if (ib, g) in mirrored:
+                nc.vector.tensor_tensor(
+                    out=a_planes[:], in0=adj_sb[b][g][:, :, i_cols], in1=dd[b, ib, g][:], op=ALU.mult
+                )
+            elif not by_row(b, ib, g):
+                for half in range(2):
+                    planes = slice(2 * half, 2 * half + 2)
+                    nc.vector.tensor_tensor(
+                        out=a_planes[:, planes, :],
+                        in0=adj_sb[b][g][:, planes, i_cols],
+                        in1=dd[b, ib, g, half][:],
+                        op=ALU.mult,
+                    )
+            for t in range(PACK) if by_row(b, ib, g) else ():
                 r = PACK * g + t
                 nc.vector.scalar_tensor_tensor(
                     out=a_planes[:, t, :],
@@ -237,26 +326,27 @@ def tile_perception_pa_kernel(tc, batch_graph, adj, W1, b1, out):
                     op1=ALU.mult,
                 )
             a_grouped[b, ib, g] = rows3.tile([P, BLOCK, PACK], BF16, align_bytes=64, name="a_grouped")
-            side_by_side(nc.scalar.copy, a_grouped[b, ib, g][:], a_planes[:])
+            copy = nc.vector.tensor_copy if (BLOCKS * ib + g) % 8 == 3 else nc.scalar.copy
+            side_by_side(copy, a_grouped[b, ib, g][:], a_planes[:])
 
         def quantise_and_multiply(b, ib, g):
+            a_codes = codes.tile([P, BLOCK], U32, align_bytes=64)
+            a_scales = codes.tile([P, BLOCK], U8, align_bytes=64)
             if g == 0:
-                a_codes[b, ib] = codes.tile([P, PASSES, BLOCK], U32, align_bytes=64, name="a_codes")
-                a_scales[b, ib] = codes.tile([P, PASSES, BLOCK], U8, align_bytes=64, name="a_scales")
                 acc[b, ib] = [
                     sums.tile([P, HIDDEN], F32, name="acc%d" % m, tag="acc") for m in range(ROW_TILES)
                 ]
             nc.vector.quantize_mx(
-                out=a_codes[b, ib][:, g, :].bitcast(FP8X4),
-                scales=a_scales[b, ib][:, g, :],
+                out=a_codes[:].bitcast(FP8X4),
+                scales=a_scales[:],
                 in_=a_grouped[b, ib, g][:].rearrange("p i t -> p (i t)"),
             )
             for m in range(ROW_TILES):
                 m_cols = slice(P * m, P * (m + 1))
                 nc.tensor.matmul_mx(
                     out=acc[b, ib][m][:],
-                    lhsT=a_codes[b, ib][:, g, m_cols].bitcast(FP8X4),
-                    lhsT_scale=a_scales[b, ib][:, g, m_cols],
+                    lhsT=a_codes[:, m_cols].bitcast(FP8X4),
+                    lhsT_scale=a_scales[:, m_cols],
                     rhs=z_codes[b][:, g, :].bitcast(FP8X4),
                     rhs_scale=z_scales[b][:, g, :],
                     start=(g == 0),
@@ -272,14 +362,17 @@ def tile_perception_pa_kernel(tc, batch_graph, adj, W1, b1, out):
                 nc.sync.dma_start(out=out[b, row0 : row0 + P, :], in_=y[:])
 
         steps = [(b, ib, g) for b in range(GRAPHS) for ib in range(BLOCKS) for g in range(PASSES)]
+        make_factors(*steps[0])
         for n, (b, ib, g) in enumerate(steps):
             scale(b, ib, g)
+            if n + 1 < len(steps):
+                make_factors(*steps[n + 1])
             if n >= 2 and steps[n - 2][2] == PASSES - 1:
                 finish(*steps[n - 2][:2])
             if n >= 1:
                 quantise_and_multiply(*steps[n - 1])
-            piece = n % STEPS - (STEPS - DEGREE_PIECES)
-            if b + 1 < GRAPHS and piece >= 0:
+            piece = n % STEPS - (STEPS - 1 - DEGREE_PIECES)
+            if b + 1 < GRAPHS and 0 <= piece < DEGREE_PIECES:
                 degree_piece(b + 1, piece)
         quantise_and_multiply(*steps[-1])
         finish(*steps[-1][:2])

@@ -311,8 +311,8 @@ def tile_perception_pa_kernel(tc, batch_graph, adj, W1, b1, out):
                     planes = slice(2 * half, 2 * half + 2)
                     nc.vector.tensor_tensor(
                         out=a_planes[:, planes, :],
-                        in0=adj_sb[b][g][:, planes, i_cols],
-                        in1=dd[b, ib, g, half][:],
+                        in0=dd[b, ib, g, half][:],
+                        in1=adj_sb[b][g][:, planes, i_cols],
                         op=ALU.mult,
                     )
             for t in range(PACK) if by_row(b, ib, g) else ():

@@ -24,8 +24,8 @@ ROW_TILES = BLOCK // P
 STEPS = BLOCKS * PASSES
 HALF = CHUNKS // 2
 SUM_PIECES = 2 * PASSES
-DEGREE_PIECES = SUM_PIECES + 6
 PARTS = 3
+LEFT_STEP = 16
 TERMS = PARTS * PARTS
 
 FLOPS = 2 * GRAPHS * NODES * FEATS * HIDDEN + 2 * GRAPHS * NODES * NODES * HIDDEN
@@ -41,7 +41,9 @@ def side_by_side(copy, grouped, planes):
 def tile_perception_pa_kernel(tc, batch_graph, adj, W1, b1, out):
     nc = tc.nc
     with ExitStack() as ctx:
+        ctx.enter_context(tc.manual_schedule())
         keep = ctx.enter_context(tc.tile_pool(name="keep", bufs=1))
+        groups_of_4 = ctx.enter_context(tc.tile_pool(name="groups_of_4", bufs=4))
         degrees = ctx.enter_context(tc.psum_pool(name="degrees", bufs=1))
 
         ident = keep.tile([P, P], F32)
@@ -109,7 +111,7 @@ def tile_perception_pa_kernel(tc, batch_graph, adj, W1, b1, out):
 
             def features_to_codes(b, g):
                 x_words = x_sb[b, g][:].bitcast(F32)
-                x_grouped = rows1.tile([P, K_PASS, PACK], BF16, align_bytes=64)
+                x_grouped = groups_of_4.tile([P, K_PASS, PACK], BF16, align_bytes=64, name="grouped")
                 x_grouped_words = x_grouped[:].bitcast(F32)
                 for half in range(2):
                     xt = work.tile([P, 2, 2, P], F32, tag="work")
@@ -135,7 +137,7 @@ def tile_perception_pa_kernel(tc, batch_graph, adj, W1, b1, out):
                 )
 
             def project(b, g):
-                z_grouped = rows1.tile([P, HIDDEN, PACK], BF16, align_bytes=64)
+                z_grouped = groups_of_4.tile([P, HIDDEN, PACK], BF16, align_bytes=64, name="grouped")
                 for hb in range(HIDDEN // P):
                     h_cols = slice(P * hb, P * (hb + 1))
                     z_ps = work.tile([P, PACK, P], F32, tag="work")
@@ -171,9 +173,9 @@ def tile_perception_pa_kernel(tc, batch_graph, adj, W1, b1, out):
 
         late = ctx.enter_context(tc.tile_pool(name="late", bufs=1))
         d_row = {}
-        d_left = [late.tile([P, NODES], BF16, name="d_left%d" % b) for b in range(GRAPHS)]
-        d_right = [late.tile([P, NODES], BF16, name="d_right%d" % b) for b in range(GRAPHS)]
-        left_cols = late.tile([P, CHUNKS, P], BF16)
+        d_left = {}
+        d_right = {}
+        left_cols = late.tile([P, CHUNKS * LEFT_STEP + P - LEFT_STEP], BF16)
         right_cols = late.tile([P, CHUNKS, P], BF16)
         nc.gpsimd.memset(left_cols[:], 0.0)
         nc.gpsimd.memset(right_cols[:], 0.0)
@@ -185,194 +187,287 @@ def tile_perception_pa_kernel(tc, batch_graph, adj, W1, b1, out):
         rest = [keep.tile([P, CHUNKS], F32, name="rest%d" % b) for b in range(GRAPHS)]
         parts = [keep.tile([P, CHUNKS, PARTS], BF16, name="parts%d" % b) for b in range(GRAPHS)]
 
-        def degree_piece(b, piece):
-            if piece < SUM_PIECES:
-                g, half = divmod(piece, 2)
-                if piece == 0:
-                    c_ps[b] = degrees.tile([P, PASSES, CHUNKS], F32, tag="degrees", name="c_ps")
-                for m in range(HALF * half, HALF * (half + 1)):
-                    for t in range(PACK):
-                        nc.tensor.matmul(
-                            out=c_ps[b][:, g, m : m + 1],
-                            lhsT=adj_sb[b][g][:, t, P * m : P * (m + 1)],
-                            rhs=ones[:, 0:1],
-                            start=(t == 0),
-                            stop=(t == PACK - 1),
-                        )
-            elif piece == SUM_PIECES:
-                nc.vector.tensor_reduce(
-                    out=c[b][:],
-                    in_=c_ps[b][:].rearrange("p g m -> p m g"),
-                    axis=mybir.AxisListType.X,
-                    op=ALU.add,
-                )
-                nc.vector.tensor_scalar_max(out=root[b][:], in0=c[b][:], scalar1=1e-30)
-                nc.scalar.activation(out=root[b][:], in_=root[b][:], func=ACT.Sqrt)
-            elif piece == SUM_PIECES + 1:
-                nc.vector.reciprocal(out=root[b][:], in_=root[b][:])
-                nc.vector.scalar_tensor_tensor(
-                    out=d_col[b][:], in0=c[b][:], scalar=0.0, in1=root[b][:], op0=ALU.is_gt, op1=ALU.mult
-                )
-                nc.vector.tensor_copy(out=parts[b][:, :, 0], in_=d_col[b][:])
-                nc.vector.tensor_sub(out=rest[b][:], in0=d_col[b][:], in1=parts[b][:, :, 0])
-                nc.vector.tensor_copy(out=parts[b][:, :, 1], in_=rest[b][:])
-                nc.vector.tensor_sub(out=rest[b][:], in0=rest[b][:], in1=parts[b][:, :, 1])
-                nc.vector.tensor_copy(out=parts[b][:, :, 2], in_=rest[b][:])
-                nc.vector.tensor_copy(
-                    out=left_cols[:, :, :TERMS].rearrange("p r (u v) -> p r u v", v=PARTS),
-                    in_=parts[b][:].unsqueeze(3).to_broadcast([P, CHUNKS, PARTS, PARTS]),
-                )
-                nc.vector.tensor_copy(
-                    out=right_cols[:, :, :TERMS].rearrange("p r (u v) -> p r u v", v=PARTS),
-                    in_=parts[b][:].unsqueeze(2).to_broadcast([P, CHUNKS, PARTS, PARTS]),
-                )
-            elif piece < SUM_PIECES + 4:
-                cols, rows = ((left_cols, d_left[b]), (right_cols, d_right[b]))[piece - SUM_PIECES - 2]
-                for h in range(2):
-                    bank = spread.tile([P, HALF, P], BF16, tag="spread", name="bank")
-                    for m in range(HALF):
-                        nc.tensor.transpose(bank[:, m, :], cols[:, HALF * h + m, :], ident_bf[:])
-                    nc.scalar.copy(
-                        out=rows[:, P * HALF * h : P * HALF * (h + 1)], in_=bank[:].rearrange("p m n -> p (m n)")
+        def sum_columns(b, piece):
+            g, half = divmod(piece, 2)
+            if piece == 0:
+                c_ps[b] = degrees.tile([P, PASSES, CHUNKS], F32, tag="degrees", name="c_ps")
+            for m in range(HALF * half, HALF * (half + 1)):
+                for t in range(PACK):
+                    nc.tensor.matmul(
+                        out=c_ps[b][:, g, m : m + 1],
+                        lhsT=adj_sb[b][g][:, t, P * m : P * (m + 1)],
+                        rhs=ones[:, 0:1],
+                        start=(t == 0),
+                        stop=(t == PACK - 1),
                     )
-            else:
-                if piece == SUM_PIECES + 4:
-                    d_row[b] = late.tile([P, NODES], F32, name="d_row")
-                for q in range(2 * (piece - SUM_PIECES - 4), 2 * (piece - SUM_PIECES - 3)):
-                    d_ps = spread.tile([P, BLOCK], F32, tag="spread", name="d_ps")
-                    for m in range(ROW_TILES):
-                        r = ROW_TILES * q + m
-                        nc.tensor.transpose(
-                            d_ps[:, P * m : P * (m + 1)],
-                            d_col[b][:, r : r + 1].to_broadcast([P, P]),
-                            ident[:],
-                        )
-                    nc.scalar.copy(out=d_row[b][:, BLOCK * q : BLOCK * (q + 1)], in_=d_ps[:])
 
-        for piece in range(DEGREE_PIECES):
-            degree_piece(0, piece)
+        def take_root(b):
+            nc.vector.tensor_reduce(
+                out=c[b][:],
+                in_=c_ps[b][:].rearrange("p g m -> p m g"),
+                axis=mybir.AxisListType.X,
+                op=ALU.add,
+            )
+            nc.vector.tensor_scalar_max(out=root[b][:], in0=c[b][:], scalar1=1e-30)
+            nc.scalar.activation(out=root[b][:], in_=root[b][:], func=ACT.Sqrt)
 
-        planes3 = ctx.enter_context(tc.tile_pool(name="planes3", bufs=2))
-        rows3 = ctx.enter_context(tc.tile_pool(name="rows3", bufs=3))
+        def invert(b):
+            nc.vector.reciprocal(out=root[b][:], in_=root[b][:])
+            nc.vector.scalar_tensor_tensor(
+                out=d_col[b][:], in0=c[b][:], scalar=0.0, in1=root[b][:], op0=ALU.is_gt, op1=ALU.mult
+            )
+
+        def split(b):
+            eng = nc.gpsimd
+            eng.tensor_copy(out=parts[b][:, :, 0], in_=d_col[b][:])
+            eng.tensor_sub(out=rest[b][:], in0=d_col[b][:], in1=parts[b][:, :, 0])
+            eng.tensor_copy(out=parts[b][:, :, 1], in_=rest[b][:])
+            eng.tensor_sub(out=rest[b][:], in0=rest[b][:], in1=parts[b][:, :, 1])
+            eng.tensor_copy(out=parts[b][:, :, 2], in_=rest[b][:])
+            eng.tensor_copy(
+                out=left_cols[:, : CHUNKS * LEFT_STEP]
+                .rearrange("p (r k) -> p r k", k=LEFT_STEP)[:, :, :TERMS]
+                .rearrange("p r (u v) -> p r u v", v=PARTS),
+                in_=parts[b][:].unsqueeze(3).to_broadcast([P, CHUNKS, PARTS, PARTS]),
+            )
+            eng.tensor_copy(
+                out=right_cols[:, :, :TERMS].rearrange("p r (u v) -> p r u v", v=PARTS),
+                in_=parts[b][:].unsqueeze(2).to_broadcast([P, CHUNKS, PARTS, PARTS]),
+            )
+            d_left[b] = late.tile([P, NODES], BF16, name="d_left", bufs=2)
+            d_right[b] = late.tile([P, NODES], BF16, name="d_right", bufs=2)
+
+        def turn_parts(b, h, left):
+            pool, tag = (spread, "spread") if b == 0 else (degrees, "degrees")
+            bank = pool.tile([P, HALF, P], BF16, tag=tag, name="bank")
+            for m in range(HALF):
+                r = HALF * h + m
+                window = left_cols[:, LEFT_STEP * r : LEFT_STEP * r + P] if left else right_cols[:, r, :]
+                nc.tensor.transpose(bank[:, m, :], window, ident_bf[:])
+            banks[b, h, left] = bank
+
+        def keep_parts(b, h, left):
+            rows = d_left[b] if left else d_right[b]
+            nc.scalar.copy(
+                out=rows[:, P * HALF * h : P * HALF * (h + 1)], in_=banks[b, h, left][:].rearrange("p m n -> p (m n)")
+            )
+
+        banks = {}
+
+        def turn_row(b, q):
+            if b not in d_row:
+                d_row[b] = late.tile([P, NODES], F32, name="d_row")
+            pool, tag = (spread, "spread") if b == 0 else (degrees, "degrees")
+            banks[b, q] = pool.tile([P, BLOCK], F32, tag=tag, name="d_ps")
+            for m in range(ROW_TILES):
+                r = ROW_TILES * q + m
+                nc.tensor.transpose(
+                    banks[b, q][:, P * m : P * (m + 1)],
+                    d_col[b][:, r : r + 1].to_broadcast([P, P]),
+                    ident[:],
+                )
+
+        def keep_row(b, q):
+            nc.scalar.copy(out=d_row[b][:, BLOCK * q : BLOCK * (q + 1)], in_=banks[b, q][:])
+
+        for piece in range(SUM_PIECES):
+            sum_columns(0, piece)
+        take_root(0)
+        invert(0)
+        turn_row(0, 0)
+        keep_row(0, 0)
+        split(0)
+        a_grouped = {}
+        a_codes = {}
+        a_scales = {}
+        planes3 = ctx.enter_context(tc.tile_pool(name="planes3", bufs=3))
         factors = ctx.enter_context(tc.tile_pool(name="factors", bufs=3))
         codes = ctx.enter_context(tc.tile_pool(name="codes", bufs=3))
-        outs = ctx.enter_context(tc.tile_pool(name="outs", bufs=6))
-        a_grouped = {}
+        outs = ctx.enter_context(tc.tile_pool(name="outs", bufs=5))
+        a_planes = {}
         acc = {}
+        y = {}
         dd = {}
+        twins = ((0, 3), (1, 2), (1, 3), (2, 3))
 
-        mirrored = ((0, 1), (0, 2), (1, 2), (2, 3))
+        def kind(b, ib, g):
+            if (b, ib, g) == (0, 0, 0):
+                return "row"
+            if (ib, g) in twins:
+                return "twin"
+            if (g, ib) in twins:
+                return "mirror"
+            return "outer"
 
-        def make_factors(b, ib, g):
-            i_cols = slice(BLOCK * ib, BLOCK * (ib + 1))
-            if (ib, g) in mirrored:
-                dd[b, ib, g] = factors.tile([P, PACK, BLOCK], BF16, name="dd_sb")
-                for t in range(PACK):
-                    r = PACK * g + t
-                    nc.vector.tensor_scalar_mul(
-                        out=dd[b, ib, g][:, t, :], in0=d_row[b][:, i_cols], scalar1=d_col[b][:, r : r + 1]
-                    )
-            elif (g, ib) in mirrored:
-                for half in range(2):
-                    dd[b, ib, g, half] = spread.tile([P, 2, BLOCK], BF16, tag="spread", name="dd")
-                    for e in range(2):
-                        t = 2 * half + e
-                        for m in range(ROW_TILES):
-                            nc.tensor.transpose(
-                                dd[b, ib, g, half][:, e, P * m : P * (m + 1)],
-                                dd[b, g, ib][:, m, P * t : P * (t + 1)],
-                                ident_bf[:],
-                            )
-            elif not by_row(b, ib, g):
-                for half in range(2):
-                    dd[b, ib, g, half] = spread.tile([P, 2, BLOCK], BF16, tag="spread", name="dd")
-                    for e in range(2):
-                        r = PACK * g + 2 * half + e
-                        nc.tensor.matmul(
-                            out=dd[b, ib, g, half][:, e, :],
-                            lhsT=d_left[b][:, P * r : P * (r + 1)],
-                            rhs=d_right[b][:, i_cols],
-                            start=True,
-                            stop=True,
+        def on_vector(n):
+            return n % 8 == 3
+
+        def twin_factors(b, ib, g):
+            dd[b, ib, g] = factors.tile([P, PACK, BLOCK], BF16, name="dd_sb")
+            for t in range(PACK):
+                r = PACK * g + t
+                nc.vector.tensor_scalar_mul(
+                    out=dd[b, ib, g][:, t, :],
+                    in0=d_row[b][:, BLOCK * ib : BLOCK * (ib + 1)],
+                    scalar1=d_col[b][:, r : r + 1],
+                )
+
+        def factor_bank(b, ib, g, half):
+            k = kind(b, ib, g)
+            if k == "mirror":
+                bank = spread.tile([P, 2, BLOCK], BF16, tag="spread", name="dd")
+                for e in range(2):
+                    t = 2 * half + e
+                    for m in range(ROW_TILES):
+                        nc.tensor.transpose(
+                            bank[:, e, P * m : P * (m + 1)], dd[b, g, ib][:, m, P * t : P * (t + 1)], ident_bf[:]
                         )
-
-        def by_row(b, ib, g):
-            return b == GRAPHS - 1 and ib == g == BLOCKS - 1
+            elif k == "outer":
+                bank = spread.tile([P, 2, BLOCK], BF16, tag="spread", name="dd")
+                for e in range(2):
+                    r = PACK * g + 2 * half + e
+                    nc.tensor.matmul(
+                        out=bank[:, e, :],
+                        lhsT=d_left[b][:, P * r : P * (r + 1)],
+                        rhs=d_right[b][:, BLOCK * ib : BLOCK * (ib + 1)],
+                        start=True,
+                        stop=True,
+                    )
+            else:
+                return
+            dd[b, ib, g, half] = bank
 
         def scale(b, ib, g):
             i_cols = slice(BLOCK * ib, BLOCK * (ib + 1))
-            a_planes = planes3.tile([P, PACK, BLOCK], BF16)
-            if (ib, g) in mirrored:
+            k = kind(b, ib, g)
+            a_planes[b, ib, g] = planes3.tile([P, PACK, BLOCK], BF16, name="a_planes")
+            if k == "row":
+                for t in range(PACK):
+                    r = PACK * g + t
+                    nc.vector.scalar_tensor_tensor(
+                        out=a_planes[b, ib, g][:, t, :],
+                        in0=adj_sb[b][g][:, t, i_cols],
+                        scalar=d_col[b][:, r : r + 1],
+                        in1=d_row[b][:, i_cols],
+                        op0=ALU.mult,
+                        op1=ALU.mult,
+                    )
+            elif k == "twin":
                 nc.vector.tensor_tensor(
-                    out=a_planes[:], in0=adj_sb[b][g][:, :, i_cols], in1=dd[b, ib, g][:], op=ALU.mult
+                    out=a_planes[b, ib, g][:], in0=adj_sb[b][g][:, :, i_cols], in1=dd[b, ib, g][:], op=ALU.mult
                 )
-            elif not by_row(b, ib, g):
+            else:
                 for half in range(2):
                     planes = slice(2 * half, 2 * half + 2)
                     nc.vector.tensor_tensor(
-                        out=a_planes[:, planes, :],
-                        in0=dd[b, ib, g, half][:],
-                        in1=adj_sb[b][g][:, planes, i_cols],
+                        out=a_planes[b, ib, g][:, planes, :],
+                        in0=adj_sb[b][g][:, planes, i_cols],
+                        in1=dd[b, ib, g, half][:],
                         op=ALU.mult,
                     )
-            for t in range(PACK) if by_row(b, ib, g) else ():
-                r = PACK * g + t
-                nc.vector.scalar_tensor_tensor(
-                    out=a_planes[:, t, :],
-                    in0=adj_sb[b][g][:, t, i_cols],
-                    scalar=d_col[b][:, r : r + 1],
-                    in1=d_row[b][:, i_cols],
-                    op0=ALU.mult,
-                    op1=ALU.mult,
-                )
-            a_grouped[b, ib, g] = rows3.tile([P, BLOCK, PACK], BF16, align_bytes=64, name="a_grouped")
-            copy = nc.vector.tensor_copy if (BLOCKS * ib + g) % 8 == 3 else nc.scalar.copy
-            side_by_side(copy, a_grouped[b, ib, g][:], a_planes[:])
 
-        def quantise_and_multiply(b, ib, g):
-            a_codes = codes.tile([P, BLOCK], U32, align_bytes=64)
-            a_scales = codes.tile([P, BLOCK], U8, align_bytes=64)
+        def regroup(b, ib, g):
+            a_grouped[b, ib, g] = groups_of_4.tile([P, BLOCK, PACK], BF16, align_bytes=64, name="grouped")
+            copy = nc.vector.tensor_copy if on_vector(BLOCKS * ib + g + 16 * b) else nc.scalar.copy
+            side_by_side(copy, a_grouped[b, ib, g][:], a_planes[b, ib, g][:])
+
+        def quantise(b, ib, g):
+            a_codes[b, ib, g] = codes.tile([P, BLOCK], U32, align_bytes=64, name="a_codes")
+            a_scales[b, ib, g] = codes.tile([P, BLOCK], U8, align_bytes=64, name="a_scales")
+            nc.vector.quantize_mx(
+                out=a_codes[b, ib, g][:].bitcast(FP8X4),
+                scales=a_scales[b, ib, g][:],
+                in_=a_grouped[b, ib, g][:].rearrange("p i t -> p (i t)"),
+            )
+
+        def multiply(b, ib, g):
             if g == 0:
                 acc[b, ib] = [
                     sums.tile([P, HIDDEN], F32, name="acc%d" % m, tag="acc") for m in range(ROW_TILES)
                 ]
-            nc.vector.quantize_mx(
-                out=a_codes[:].bitcast(FP8X4),
-                scales=a_scales[:],
-                in_=a_grouped[b, ib, g][:].rearrange("p i t -> p (i t)"),
-            )
             for m in range(ROW_TILES):
                 m_cols = slice(P * m, P * (m + 1))
                 nc.tensor.matmul_mx(
                     out=acc[b, ib][m][:],
-                    lhsT=a_codes[:, m_cols].bitcast(FP8X4),
-                    lhsT_scale=a_scales[:, m_cols],
+                    lhsT=a_codes[b, ib, g][:, m_cols].bitcast(FP8X4),
+                    lhsT_scale=a_scales[b, ib, g][:, m_cols],
                     rhs=z_codes[b][:, g, :].bitcast(FP8X4),
                     rhs_scale=z_scales[b][:, g, :],
                     start=(g == 0),
                     stop=(g == PASSES - 1),
                 )
 
-        def finish(b, ib):
-            for m in range(ROW_TILES):
-                y = outs.tile([P, HIDDEN], F32)
-                nc.vector.tensor_tensor(out=y[:], in0=acc[b, ib][m][:], in1=bias_row[:], op=ALU.add)
-                nc.scalar.activation(out=y[:], in_=y[:], func=ACT.Relu)
-                row0 = BLOCK * ib + P * m
-                nc.sync.dma_start(out=out[b, row0 : row0 + P, :], in_=y[:])
+        def add_bias(b, ib, m):
+            y[b, ib, m] = outs.tile([P, HIDDEN], F32, name="y")
+            nc.vector.tensor_tensor(out=y[b, ib, m][:], in0=acc[b, ib][m][:], in1=bias_row[:], op=ALU.add)
+
+        def rectify(b, ib, m):
+            nc.scalar.activation(out=y[b, ib, m][:], in_=y[b, ib, m][:], func=ACT.Relu)
+            row0 = BLOCK * ib + P * m
+            nc.sync.dma_start(out=out[b, row0 : row0 + P, :], in_=y[b, ib, m][:])
 
         steps = [(b, ib, g) for b in range(GRAPHS) for ib in range(BLOCKS) for g in range(PASSES)]
-        make_factors(*steps[0])
+        none = lambda: None
+        before = {}
+        after = {}
+        for q in range(1, BLOCKS):
+            after.setdefault(q - 1, []).append(lambda q=q: turn_row(0, q))
+            before.setdefault(q, []).append(lambda q=q: keep_row(0, q))
+        at = 1
+        for k in range(SUM_PIECES):
+            after.setdefault(at, []).append(lambda k=k: sum_columns(1, k))
+            at += 1
+        for job in (take_root, invert, split):
+            after.setdefault(at, []).append(lambda job=job: job(1))
+            at += 1
+        for side in [(0, True), (0, False), (1, True), (1, False)]:
+            after.setdefault(at - 1, []).append(lambda side=side: turn_parts(1, *side))
+            before.setdefault(at, []).append(lambda side=side: keep_parts(1, *side))
+            at += 1
+        for q in range(BLOCKS):
+            after.setdefault(at - 1, []).append(lambda q=q: turn_row(1, q))
+            before.setdefault(at, []).append(lambda q=q: keep_row(1, q))
+            at += 1
+        relus = []
+        todo = {}
+        for k, step in enumerate(steps):
+            if kind(*step) == "twin":
+                todo.setdefault(max(k - 3, 0), []).append(step)
+        for left in (True, False):
+            turn_parts(0, 0, left)
+            keep_parts(0, 0, left)
+        factor_bank(*steps[1], 0)
+        factor_bank(*steps[1], 1)
+        for left in (True, False):
+            turn_parts(0, 1, left)
+            keep_parts(0, 1, left)
         for n, (b, ib, g) in enumerate(steps):
             scale(b, ib, g)
-            if n + 1 < len(steps):
-                make_factors(*steps[n + 1])
-            if n >= 2 and steps[n - 2][2] == PASSES - 1:
-                finish(*steps[n - 2][:2])
-            if n >= 1:
-                quantise_and_multiply(*steps[n - 1])
-            piece = n % STEPS - (STEPS - 1 - DEGREE_PIECES)
-            if b + 1 < GRAPHS and 0 <= piece < DEGREE_PIECES:
-                degree_piece(b + 1, piece)
-        quantise_and_multiply(*steps[-1])
-        finish(*steps[-1][:2])
+            for job in before.get(n, ()):
+                job()
+            regroup(b, ib, g)
+            if n + 1 < len(steps) and n >= 1:
+                factor_bank(*steps[n + 1], 0)
+                factor_bank(*steps[n + 1], 1)
+            for job in relus[:2]:
+                rectify(*job)
+            relus = relus[2:]
+            if n >= 3 and steps[n - 3][2] == PASSES - 1:
+                for m in range(ROW_TILES):
+                    add_bias(*steps[n - 3][:2], m)
+                    relus.append((*steps[n - 3][:2], m))
+            if n >= 2:
+                quantise(*steps[n - 2])
+                multiply(*steps[n - 2])
+            for step in todo.get(n, ()):
+                twin_factors(*step)
+            for job in after.get(n, ()):
+                job()
+        for n in range(len(steps) - 2, len(steps)):
+            quantise(*steps[n])
+            multiply(*steps[n])
+        for job in relus:
+            rectify(*job)
+        for m in range(ROW_TILES):
+            add_bias(*steps[-1][:2], m)
+            rectify(*steps[-1][:2], m)

@@ -18,15 +18,13 @@ K_PASS = P * PACK
 GRAPHS, NODES, FEATS, HIDDEN = 2, 2048, 512, 512
 CHUNKS = NODES // P
 PASSES = NODES // K_PASS
-BLOCK = 512
+BLOCK = 256
 BLOCKS = NODES // BLOCK
 ROW_TILES = BLOCK // P
-STEPS = BLOCKS * PASSES
-HALF = CHUNKS // 2
-SUM_PIECES = 2 * PASSES
 PARTS = 3
 LEFT_STEP = 16
 TERMS = PARTS * PARTS
+HALF = CHUNKS // 2
 
 FLOPS = 2 * GRAPHS * NODES * FEATS * HIDDEN + 2 * GRAPHS * NODES * NODES * HIDDEN
 
@@ -43,8 +41,6 @@ def tile_perception_pa_kernel(tc, batch_graph, adj, W1, b1, out):
     with ExitStack() as ctx:
         ctx.enter_context(tc.manual_schedule())
         keep = ctx.enter_context(tc.tile_pool(name="keep", bufs=1))
-        groups_of_4 = ctx.enter_context(tc.tile_pool(name="groups_of_4", bufs=4))
-        degrees = ctx.enter_context(tc.psum_pool(name="degrees", bufs=1))
 
         ident = keep.tile([P, P], F32)
         make_identity(nc, ident[:])
@@ -71,9 +67,25 @@ def tile_perception_pa_kernel(tc, batch_graph, adj, W1, b1, out):
         d_col = [keep.tile([P, CHUNKS], F32, name="d_col%d" % b) for b in range(GRAPHS)]
         bias_row = keep.tile([P, HIDDEN], F32)
 
+        degrees = ctx.enter_context(tc.psum_pool(name="degrees", bufs=1))
+        banks = {}
+
+        def sum_columns(b, g, m0, m1):
+            if (b, "c") not in banks:
+                banks[b, "c"] = degrees.tile([P, PASSES, CHUNKS], F32, tag="degrees", name="c_ps")
+            for m in range(m0, m1):
+                for t in range(PACK):
+                    nc.tensor.matmul(
+                        out=banks[b, "c"][:, g, m : m + 1],
+                        lhsT=adj_sb[b][g][:, t, P * m : P * (m + 1)],
+                        rhs=ones[:, 0:1],
+                        start=(t == 0),
+                        stop=(t == PACK - 1),
+                    )
+
         with ExitStack() as stage1:
             feats = stage1.enter_context(tc.tile_pool(name="feats", bufs=1))
-            rows1 = stage1.enter_context(tc.tile_pool(name="rows1", bufs=2))
+            rows1 = stage1.enter_context(tc.tile_pool(name="rows1", bufs=3))
             work = stage1.enter_context(tc.psum_pool(name="work", bufs=7))
 
             w_planes = feats.tile([P, PACK, HIDDEN], BF16)
@@ -108,43 +120,51 @@ def tile_perception_pa_kernel(tc, batch_graph, adj, W1, b1, out):
 
             x_codes = {}
             x_scales = {}
+            x_grouped = {}
+            xt = {}
 
-            def features_to_codes(b, g):
+            def turn_features(b, g):
                 x_words = x_sb[b, g][:].bitcast(F32)
-                x_grouped = groups_of_4.tile([P, K_PASS, PACK], BF16, align_bytes=64, name="grouped")
-                x_grouped_words = x_grouped[:].bitcast(F32)
                 for half in range(2):
-                    xt = work.tile([P, 2, 2, P], F32, tag="work")
+                    xt[b, g, half] = work.tile([P, 2, 2, P], F32, tag="work", name="xt")
                     for c in range(2):
                         for u in range(2):
                             nc.tensor.transpose(
-                                xt[:, c, u, :],
+                                xt[b, g, half][:, c, u, :],
                                 x_words[:, 2 * half + c, P * u : P * (u + 1)],
                                 ident[:],
                             )
-                    nc.scalar.copy(
-                        out=x_grouped_words[:, 2 * P * half : 2 * P * (half + 1), :].rearrange(
-                            "p (c n) u -> p c n u", c=2
-                        ),
-                        in_=xt[:].rearrange("p c u n -> p c n u"),
+
+            def group_features(b, g):
+                x_grouped[b, g] = rows1.tile([P, K_PASS, PACK], BF16, align_bytes=64, name="x_grouped")
+                words = x_grouped[b, g][:].bitcast(F32)
+                for half in range(2):
+                    copy = nc.scalar.copy if True else nc.vector.tensor_copy
+                    copy(
+                        out=words[:, 2 * P * half : 2 * P * (half + 1), :].rearrange("p (c n) u -> p c n u", c=2),
+                        in_=xt[b, g, half][:].rearrange("p c u n -> p c n u"),
                     )
+
+            def quantise_features(b, g):
                 x_codes[b, g] = rows1.tile([P, K_PASS], U32, align_bytes=64, name="x_codes")
                 x_scales[b, g] = rows1.tile([P, K_PASS], U8, align_bytes=64, name="x_scales")
                 nc.vector.quantize_mx(
                     out=x_codes[b, g][:].bitcast(FP8X4),
                     scales=x_scales[b, g][:],
-                    in_=x_grouped[:].rearrange("p n t -> p (n t)"),
+                    in_=x_grouped[b, g][:].rearrange("p n t -> p (n t)"),
                 )
 
+            z_ps = {}
+            z_grouped = {}
+
             def project(b, g):
-                z_grouped = groups_of_4.tile([P, HIDDEN, PACK], BF16, align_bytes=64, name="grouped")
                 for hb in range(HIDDEN // P):
                     h_cols = slice(P * hb, P * (hb + 1))
-                    z_ps = work.tile([P, PACK, P], F32, tag="work")
+                    z_ps[b, g, hb] = work.tile([P, PACK, P], F32, tag="work", name="z_ps")
                     for t in range(PACK):
                         n_cols = slice(P * t, P * (t + 1))
                         nc.tensor.matmul_mx(
-                            out=z_ps[:, t, :],
+                            out=z_ps[b, g, hb][:, t, :],
                             lhsT=x_codes[b, g][:, n_cols].bitcast(FP8X4),
                             lhsT_scale=x_scales[b, g][:, n_cols],
                             rhs=w_codes[:, h_cols].bitcast(FP8X4),
@@ -152,20 +172,36 @@ def tile_perception_pa_kernel(tc, batch_graph, adj, W1, b1, out):
                             start=True,
                             stop=True,
                         )
+
+            def group_z(b, g):
+                z_grouped[b, g] = rows1.tile([P, HIDDEN, PACK], BF16, align_bytes=64, name="z_grouped")
+                for hb in range(HIDDEN // P):
+                    h_cols = slice(P * hb, P * (hb + 1))
                     copy = nc.vector.tensor_copy if hb % 2 == 0 else nc.scalar.copy
-                    copy(out=z_grouped[:, h_cols, :], in_=z_ps[:].rearrange("p t h -> p h t"))
+                    copy(out=z_grouped[b, g][:, h_cols, :], in_=z_ps[b, g, hb][:].rearrange("p t h -> p h t"))
+
+            def quantise_z(b, g):
                 nc.vector.quantize_mx(
                     out=z_codes[b][:, g, :].bitcast(FP8X4),
                     scales=z_scales[b][:, g, :],
-                    in_=z_grouped[:].rearrange("p h t -> p (h t)"),
+                    in_=z_grouped[b, g][:].rearrange("p h t -> p (h t)"),
                 )
 
             groups = [(b, g) for b in range(GRAPHS) for g in range(PASSES)]
-            for n, (b, g) in enumerate(groups):
-                features_to_codes(b, g)
-                if n >= 1:
-                    project(*groups[n - 1])
-            project(*groups[-1])
+            for n in range(len(groups) + 3):
+                if n < len(groups):
+                    turn_features(*groups[n])
+                    group_features(*groups[n])
+                if 1 <= n <= len(groups):
+                    quantise_features(*groups[n - 1])
+                if 2 <= n < len(groups) + 2:
+                    project(*groups[n - 2])
+                    group_z(*groups[n - 2])
+                if n >= 3:
+                    quantise_z(*groups[n - 3])
+                g = n - 8
+                if 0 <= g < PASSES - 1:
+                    sum_columns(0, g, 0, CHUNKS)
 
             bias_ps = work.tile([P, HIDDEN], F32, tag="work")
             nc.tensor.matmul(out=bias_ps[:], lhsT=ones[:], rhs=bias_in[:], start=True, stop=True)
@@ -179,32 +215,16 @@ def tile_perception_pa_kernel(tc, batch_graph, adj, W1, b1, out):
         right_cols = late.tile([P, CHUNKS, P], BF16)
         nc.gpsimd.memset(left_cols[:], 0.0)
         nc.gpsimd.memset(right_cols[:], 0.0)
-        sums = ctx.enter_context(tc.psum_pool(name="sums", bufs=ROW_TILES))
+        sums = ctx.enter_context(tc.psum_pool(name="sums", bufs=4))
         spread = ctx.enter_context(tc.psum_pool(name="spread", bufs=3))
-        c_ps = {}
         c = [keep.tile([P, CHUNKS], F32, name="c%d" % b) for b in range(GRAPHS)]
         root = [keep.tile([P, CHUNKS], F32, name="root%d" % b) for b in range(GRAPHS)]
         rest = [keep.tile([P, CHUNKS], F32, name="rest%d" % b) for b in range(GRAPHS)]
         parts = [keep.tile([P, CHUNKS, PARTS], BF16, name="parts%d" % b) for b in range(GRAPHS)]
-
-        def sum_columns(b, piece):
-            g, half = divmod(piece, 2)
-            if piece == 0:
-                c_ps[b] = degrees.tile([P, PASSES, CHUNKS], F32, tag="degrees", name="c_ps")
-            for m in range(HALF * half, HALF * (half + 1)):
-                for t in range(PACK):
-                    nc.tensor.matmul(
-                        out=c_ps[b][:, g, m : m + 1],
-                        lhsT=adj_sb[b][g][:, t, P * m : P * (m + 1)],
-                        rhs=ones[:, 0:1],
-                        start=(t == 0),
-                        stop=(t == PACK - 1),
-                    )
-
         def take_root(b):
             nc.vector.tensor_reduce(
                 out=c[b][:],
-                in_=c_ps[b][:].rearrange("p g m -> p m g"),
+                in_=banks[b, "c"][:].rearrange("p g m -> p m g"),
                 axis=mybir.AxisListType.X,
                 op=ALU.add,
             )
@@ -218,7 +238,7 @@ def tile_perception_pa_kernel(tc, batch_graph, adj, W1, b1, out):
             )
 
         def split(b):
-            eng = nc.gpsimd
+            eng = nc.vector if b == 0 else nc.gpsimd
             eng.tensor_copy(out=parts[b][:, :, 0], in_=d_col[b][:])
             eng.tensor_sub(out=rest[b][:], in0=d_col[b][:], in1=parts[b][:, :, 0])
             eng.tensor_copy(out=parts[b][:, :, 1], in_=rest[b][:])
@@ -234,10 +254,11 @@ def tile_perception_pa_kernel(tc, batch_graph, adj, W1, b1, out):
                 out=right_cols[:, :, :TERMS].rearrange("p r (u v) -> p r u v", v=PARTS),
                 in_=parts[b][:].unsqueeze(2).to_broadcast([P, CHUNKS, PARTS, PARTS]),
             )
-            d_left[b] = late.tile([P, NODES], BF16, name="d_left", bufs=2)
-            d_right[b] = late.tile([P, NODES], BF16, name="d_right", bufs=2)
 
         def turn_parts(b, h, left):
+            if b not in d_left:
+                d_left[b] = late.tile([P, NODES], BF16, name="d_left", bufs=2)
+                d_right[b] = late.tile([P, NODES], BF16, name="d_right", bufs=2)
             pool, tag = (spread, "spread") if b == 0 else (degrees, "degrees")
             bank = pool.tile([P, HALF, P], BF16, tag=tag, name="bank")
             for m in range(HALF):
@@ -252,90 +273,78 @@ def tile_perception_pa_kernel(tc, batch_graph, adj, W1, b1, out):
                 out=rows[:, P * HALF * h : P * HALF * (h + 1)], in_=banks[b, h, left][:].rearrange("p m n -> p (m n)")
             )
 
-        banks = {}
-
         def turn_row(b, q):
             if b not in d_row:
-                d_row[b] = late.tile([P, NODES], F32, name="d_row")
+                d_row[b] = late.tile([P, 3 * K_PASS], F32, name="d_row")
             pool, tag = (spread, "spread") if b == 0 else (degrees, "degrees")
-            banks[b, q] = pool.tile([P, BLOCK], F32, tag=tag, name="d_ps")
-            for m in range(ROW_TILES):
-                r = ROW_TILES * q + m
+            banks[b, "row", q] = pool.tile([P, K_PASS], F32, tag=tag, name="d_ps")
+            for m in range(PACK):
+                r = PACK * q + m
                 nc.tensor.transpose(
-                    banks[b, q][:, P * m : P * (m + 1)],
+                    banks[b, "row", q][:, P * m : P * (m + 1)],
                     d_col[b][:, r : r + 1].to_broadcast([P, P]),
                     ident[:],
                 )
 
         def keep_row(b, q):
-            nc.scalar.copy(out=d_row[b][:, BLOCK * q : BLOCK * (q + 1)], in_=banks[b, q][:])
+            nc.scalar.copy(out=d_row[b][:, K_PASS * q : K_PASS * (q + 1)], in_=banks[b, "row", q][:])
 
-        for piece in range(SUM_PIECES):
-            sum_columns(0, piece)
-        take_root(0)
-        invert(0)
-        turn_row(0, 0)
-        keep_row(0, 0)
-        split(0)
+        planes3 = ctx.enter_context(tc.tile_pool(name="planes3", bufs=4))
+        groups3 = ctx.enter_context(tc.tile_pool(name="groups3", bufs=5))
+        factors = ctx.enter_context(tc.tile_pool(name="factors", bufs=3))
+        codes = ctx.enter_context(tc.tile_pool(name="codes", bufs=4))
+        outs = ctx.enter_context(tc.tile_pool(name="outs", bufs=6))
+        a_planes = {}
         a_grouped = {}
         a_codes = {}
         a_scales = {}
-        planes3 = ctx.enter_context(tc.tile_pool(name="planes3", bufs=3))
-        factors = ctx.enter_context(tc.tile_pool(name="factors", bufs=3))
-        codes = ctx.enter_context(tc.tile_pool(name="codes", bufs=3))
-        outs = ctx.enter_context(tc.tile_pool(name="outs", bufs=5))
-        a_planes = {}
         acc = {}
         y = {}
         dd = {}
-        twins = ((0, 3), (1, 2), (1, 3), (2, 3))
+        twins = ((0, 1), (0, 2), (1, 2), (2, 3))
 
         def kind(b, ib, g):
-            if (b, ib, g) == (0, 0, 0):
+            if (b, ib // 2, g) == (0, 0, 0):
                 return "row"
-            if (ib, g) in twins:
+            if (ib // 2, g) in twins:
                 return "twin"
-            if (g, ib) in twins:
+            if (g, ib // 2) in twins:
                 return "mirror"
             return "outer"
 
-        def on_vector(n):
-            return n % 8 == 3
-
-        def twin_factors(b, ib, g):
-            dd[b, ib, g] = factors.tile([P, PACK, BLOCK], BF16, name="dd_sb")
+        def twin_factors(b, block, g):
+            dd[b, block, g] = factors.tile([P, PACK, K_PASS], BF16, name="dd_sb")
             for t in range(PACK):
                 r = PACK * g + t
                 nc.vector.tensor_scalar_mul(
-                    out=dd[b, ib, g][:, t, :],
-                    in0=d_row[b][:, BLOCK * ib : BLOCK * (ib + 1)],
+                    out=dd[b, block, g][:, t, :],
+                    in0=d_row[b][:, K_PASS * block : K_PASS * (block + 1)],
                     scalar1=d_col[b][:, r : r + 1],
                 )
 
-        def factor_bank(b, ib, g, half):
+        def factor_bank(b, ib, g):
             k = kind(b, ib, g)
-            if k == "mirror":
-                bank = spread.tile([P, 2, BLOCK], BF16, tag="spread", name="dd")
-                for e in range(2):
-                    t = 2 * half + e
+            if k in ("row", "twin"):
+                return
+            bank = spread.tile([P, PACK, BLOCK], BF16, tag="spread", name="dd")
+            dd[b, ib, g, "bank"] = bank
+            for t in range(PACK):
+                if k == "mirror":
                     for m in range(ROW_TILES):
                         nc.tensor.transpose(
-                            bank[:, e, P * m : P * (m + 1)], dd[b, g, ib][:, m, P * t : P * (t + 1)], ident_bf[:]
+                            bank[:, t, P * m : P * (m + 1)],
+                            dd[b, g, ib // 2][:, ROW_TILES * (ib % 2) + m, P * t : P * (t + 1)],
+                            ident_bf[:],
                         )
-            elif k == "outer":
-                bank = spread.tile([P, 2, BLOCK], BF16, tag="spread", name="dd")
-                for e in range(2):
-                    r = PACK * g + 2 * half + e
+                else:
+                    r = PACK * g + t
                     nc.tensor.matmul(
-                        out=bank[:, e, :],
+                        out=bank[:, t, :],
                         lhsT=d_left[b][:, P * r : P * (r + 1)],
                         rhs=d_right[b][:, BLOCK * ib : BLOCK * (ib + 1)],
                         start=True,
                         stop=True,
                     )
-            else:
-                return
-            dd[b, ib, g, half] = bank
 
         def scale(b, ib, g):
             i_cols = slice(BLOCK * ib, BLOCK * (ib + 1))
@@ -352,23 +361,20 @@ def tile_perception_pa_kernel(tc, batch_graph, adj, W1, b1, out):
                         op0=ALU.mult,
                         op1=ALU.mult,
                     )
-            elif k == "twin":
-                nc.vector.tensor_tensor(
-                    out=a_planes[b, ib, g][:], in0=adj_sb[b][g][:, :, i_cols], in1=dd[b, ib, g][:], op=ALU.mult
-                )
+                return
+            if k == "twin":
+                half = BLOCK * (ib % 2)
+                by = dd[b, ib // 2, g][:, :, half : half + BLOCK]
             else:
-                for half in range(2):
-                    planes = slice(2 * half, 2 * half + 2)
-                    nc.vector.tensor_tensor(
-                        out=a_planes[b, ib, g][:, planes, :],
-                        in0=adj_sb[b][g][:, planes, i_cols],
-                        in1=dd[b, ib, g, half][:],
-                        op=ALU.mult,
-                    )
+                by = dd[b, ib, g, "bank"][:]
+            nc.vector.tensor_tensor(out=a_planes[b, ib, g][:], in0=adj_sb[b][g][:, :, i_cols], in1=by, op=ALU.mult)
 
-        def regroup(b, ib, g):
-            a_grouped[b, ib, g] = groups_of_4.tile([P, BLOCK, PACK], BF16, align_bytes=64, name="grouped")
-            copy = nc.vector.tensor_copy if on_vector(BLOCKS * ib + g + 16 * b) else nc.scalar.copy
+        def on_vector(k):
+            return k % 16 == 7
+
+        def regroup(b, ib, g, k):
+            a_grouped[b, ib, g] = groups3.tile([P, BLOCK, PACK], BF16, align_bytes=64, name="a_grouped")
+            copy = nc.vector.tensor_copy if on_vector(k) else nc.scalar.copy
             side_by_side(copy, a_grouped[b, ib, g][:], a_planes[b, ib, g][:])
 
         def quantise(b, ib, g):
@@ -382,9 +388,7 @@ def tile_perception_pa_kernel(tc, batch_graph, adj, W1, b1, out):
 
         def multiply(b, ib, g):
             if g == 0:
-                acc[b, ib] = [
-                    sums.tile([P, HIDDEN], F32, name="acc%d" % m, tag="acc") for m in range(ROW_TILES)
-                ]
+                acc[b, ib] = [sums.tile([P, HIDDEN], F32, name="acc%d" % m, tag="acc") for m in range(ROW_TILES)]
             for m in range(ROW_TILES):
                 m_cols = slice(P * m, P * (m + 1))
                 nc.tensor.matmul_mx(
@@ -407,65 +411,86 @@ def tile_perception_pa_kernel(tc, batch_graph, adj, W1, b1, out):
             nc.sync.dma_start(out=out[b, row0 : row0 + P, :], in_=y[b, ib, m][:])
 
         steps = [(b, ib, g) for b in range(GRAPHS) for ib in range(BLOCKS) for g in range(PASSES)]
-        none = lambda: None
+        N = len(steps)
+        HALFWAY = N // 2
         before = {}
         after = {}
-        for q in range(1, BLOCKS):
-            after.setdefault(q - 1, []).append(lambda q=q: turn_row(0, q))
-            before.setdefault(q, []).append(lambda q=q: keep_row(0, q))
+
+        def ride(at, first, second=None):
+            after.setdefault(at, []).append(first)
+            if second:
+                before.setdefault(at + 1, []).append(second)
+
+        sum_columns(0, PASSES - 1, 0, CHUNKS)
+        take_root(0)
+        invert(0)
+        turn_row(0, 0)
+        keep_row(0, 0)
+        split(0)
+        for h, left in ((1, True), (0, False)):
+            turn_parts(0, h, left)
+            keep_parts(0, h, left)
+
+        ride(0, lambda: turn_parts(0, 0, True), lambda: keep_parts(0, 0, True))
+        ride(2, lambda: turn_parts(0, 1, False), lambda: keep_parts(0, 1, False))
+        ride(4, lambda: turn_row(0, 1), lambda: keep_row(0, 1))
+        ride(6, lambda: turn_row(0, 2), lambda: keep_row(0, 2))
         at = 1
-        for k in range(SUM_PIECES):
-            after.setdefault(at, []).append(lambda k=k: sum_columns(1, k))
-            at += 1
+        for g in range(PASSES):
+            for q in range(4):
+                m0 = 4 * q
+                ride(at, lambda g=g, m0=m0: sum_columns(1, g, m0, m0 + 4))
+                at += 1
         for job in (take_root, invert, split):
-            after.setdefault(at, []).append(lambda job=job: job(1))
+            after.setdefault(at + 1, []).append(lambda job=job: job(1))
             at += 1
-        for side in [(0, True), (0, False), (1, True), (1, False)]:
-            after.setdefault(at - 1, []).append(lambda side=side: turn_parts(1, *side))
-            before.setdefault(at, []).append(lambda side=side: keep_parts(1, *side))
+        at += 3
+        for h, left in ((0, True), (0, False), (1, True), (1, False)):
+            ride(at, lambda h=h, left=left: turn_parts(1, h, left), lambda h=h, left=left: keep_parts(1, h, left))
             at += 1
-        for q in range(BLOCKS):
-            after.setdefault(at - 1, []).append(lambda q=q: turn_row(1, q))
-            before.setdefault(at, []).append(lambda q=q: keep_row(1, q))
+        for q in range(3):
+            ride(at, lambda q=q: turn_row(1, q), lambda q=q: keep_row(1, q))
             at += 1
-        relus = []
+        assert at <= HALFWAY, at
+
         todo = {}
-        for k, step in enumerate(steps):
-            if kind(*step) == "twin":
-                todo.setdefault(max(k - 3, 0), []).append(step)
-        for left in (True, False):
-            turn_parts(0, 0, left)
-            keep_parts(0, 0, left)
-        factor_bank(*steps[1], 0)
-        factor_bank(*steps[1], 1)
-        for left in (True, False):
-            turn_parts(0, 1, left)
-            keep_parts(0, 1, left)
-        for n, (b, ib, g) in enumerate(steps):
+        for k, (b, ib, g) in enumerate(steps):
+            if kind(b, ib, g) == "twin" and ib % 2 == 0:
+                todo.setdefault(max(k - 3, 0), []).append((b, ib // 2, g))
+
+        adds = []
+        relus = []
+        for k in range(1, 3):
+            factor_bank(*steps[k])
+        for k, (b, ib, g) in enumerate(steps):
             scale(b, ib, g)
-            for job in before.get(n, ()):
+            for job in before.get(k, ()):
                 job()
-            regroup(b, ib, g)
-            if n + 1 < len(steps) and n >= 1:
-                factor_bank(*steps[n + 1], 0)
-                factor_bank(*steps[n + 1], 1)
-            for job in relus[:2]:
-                rectify(*job)
-            relus = relus[2:]
-            if n >= 3 and steps[n - 3][2] == PASSES - 1:
-                for m in range(ROW_TILES):
-                    add_bias(*steps[n - 3][:2], m)
-                    relus.append((*steps[n - 3][:2], m))
-            if n >= 2:
-                quantise(*steps[n - 2])
-                multiply(*steps[n - 2])
-            for step in todo.get(n, ()):
+            regroup(b, ib, g, k)
+            if k + 3 < N:
+                factor_bank(*steps[k + 3])
+            if relus:
+                rectify(*relus.pop(0))
+            if adds and k >= adds[0][0]:
+                job = adds.pop(0)[1]
+                add_bias(*job)
+                relus.append(job)
+            if k >= 3:
+                quantise(*steps[k - 3])
+                multiply(*steps[k - 3])
+                if steps[k - 3][2] == PASSES - 1:
+                    for m in range(ROW_TILES):
+                        adds.append((k + 2, (*steps[k - 3][:2], m)))
+            for step in todo.get(k, ()):
                 twin_factors(*step)
-            for job in after.get(n, ()):
+            for job in after.get(k, ()):
                 job()
-        for n in range(len(steps) - 2, len(steps)):
-            quantise(*steps[n])
-            multiply(*steps[n])
+        for k in range(N - 3, N):
+            quantise(*steps[k])
+            multiply(*steps[k])
+        for at, job in adds:
+            add_bias(*job)
+            relus.append(job)
         for job in relus:
             rectify(*job)
         for m in range(ROW_TILES):

@@ -70,17 +70,17 @@ def tile_perception_pa_kernel(tc, batch_graph, adj, W1, b1, out):
         degrees = ctx.enter_context(tc.psum_pool(name="degrees", bufs=1))
         banks = {}
 
-        def sum_columns(b, g, m0, m1):
+        def sum_columns(b, g, m0, m1, planes=range(PACK), part=None):
             if (b, "c") not in banks:
-                banks[b, "c"] = degrees.tile([P, PASSES, CHUNKS], F32, tag="degrees", name="c_ps")
+                banks[b, "c"] = degrees.tile([P, PASSES + 1, CHUNKS], F32, tag="degrees", name="c_ps")
             for m in range(m0, m1):
-                for t in range(PACK):
+                for t in planes:
                     nc.tensor.matmul(
-                        out=banks[b, "c"][:, g, m : m + 1],
+                        out=banks[b, "c"][:, g if part is None else part, m : m + 1],
                         lhsT=adj_sb[b][g][:, t, P * m : P * (m + 1)],
                         rhs=ones[:, 0:1],
-                        start=(t == 0),
-                        stop=(t == PACK - 1),
+                        start=(t == planes[0]),
+                        stop=(t == planes[-1]),
                     )
 
         with ExitStack() as stage1:
@@ -106,7 +106,11 @@ def tile_perception_pa_kernel(tc, batch_graph, adj, W1, b1, out):
             for b in range(GRAPHS):
                 adj_chunks = adj[b].rearrange("(r p) i -> p r i", p=P)
                 for g in range(PASSES):
-                    nc.sync.dma_start(out=adj_sb[b][g][:], in_=adj_chunks[:, PACK * g : PACK * (g + 1), :])
+                    for t in (0, 2) if (b, g) == (0, PASSES - 1) else (0,):
+                        w = 2 if (b, g) == (0, PASSES - 1) else PACK
+                        nc.sync.dma_start(
+                            out=adj_sb[b][g][:, t : t + w, :], in_=adj_chunks[:, PACK * g + t : PACK * g + t + w, :]
+                        )
 
             w_grouped = feats.tile([P, HIDDEN, PACK], BF16, align_bytes=64)
             side_by_side(nc.vector.tensor_copy, w_grouped[:], w_planes[:])
@@ -199,13 +203,14 @@ def tile_perception_pa_kernel(tc, batch_graph, adj, W1, b1, out):
                     group_z(*groups[n - 2])
                 if n >= 3:
                     quantise_z(*groups[n - 3])
-                g = n - 8
+                if n == 5:
+                    bias_ps = work.tile([P, HIDDEN], F32, tag="work")
+                    nc.tensor.matmul(out=bias_ps[:], lhsT=ones[:], rhs=bias_in[:], start=True, stop=True)
+                    nc.vector.tensor_copy(out=bias_row[:], in_=bias_ps[:])
+                g = n - 7
                 if 0 <= g < PASSES - 1:
                     sum_columns(0, g, 0, CHUNKS)
 
-            bias_ps = work.tile([P, HIDDEN], F32, tag="work")
-            nc.tensor.matmul(out=bias_ps[:], lhsT=ones[:], rhs=bias_in[:], start=True, stop=True)
-            nc.vector.tensor_copy(out=bias_row[:], in_=bias_ps[:])
 
         late = ctx.enter_context(tc.tile_pool(name="late", bufs=1))
         d_row = {}
@@ -224,12 +229,11 @@ def tile_perception_pa_kernel(tc, batch_graph, adj, W1, b1, out):
         def take_root(b):
             nc.vector.tensor_reduce(
                 out=c[b][:],
-                in_=banks[b, "c"][:].rearrange("p g m -> p m g"),
+                in_=banks[b, "c"][:, : PASSES + 1 - b, :].rearrange("p g m -> p m g"),
                 axis=mybir.AxisListType.X,
                 op=ALU.add,
             )
-            nc.vector.tensor_scalar_max(out=root[b][:], in0=c[b][:], scalar1=1e-30)
-            nc.scalar.activation(out=root[b][:], in_=root[b][:], func=ACT.Sqrt)
+            nc.scalar.activation(out=root[b][:], in_=c[b][:], func=ACT.Sqrt, bias=1e-30)
 
         def invert(b):
             nc.vector.reciprocal(out=root[b][:], in_=root[b][:])
@@ -370,7 +374,7 @@ def tile_perception_pa_kernel(tc, batch_graph, adj, W1, b1, out):
             nc.vector.tensor_tensor(out=a_planes[b, ib, g][:], in0=adj_sb[b][g][:, :, i_cols], in1=by, op=ALU.mult)
 
         def on_vector(k):
-            return k % 16 == 7
+            return k % 8 == 3
 
         def regroup(b, ib, g, k):
             a_grouped[b, ib, g] = groups3.tile([P, BLOCK, PACK], BF16, align_bytes=64, name="a_grouped")
@@ -421,7 +425,8 @@ def tile_perception_pa_kernel(tc, batch_graph, adj, W1, b1, out):
             if second:
                 before.setdefault(at + 1, []).append(second)
 
-        sum_columns(0, PASSES - 1, 0, CHUNKS)
+        sum_columns(0, PASSES - 1, 0, CHUNKS, range(2))
+        sum_columns(0, PASSES - 1, 0, CHUNKS, range(2, PACK), PASSES)
         take_root(0)
         invert(0)
         turn_row(0, 0)
@@ -429,13 +434,16 @@ def tile_perception_pa_kernel(tc, batch_graph, adj, W1, b1, out):
         split(0)
         for h, left in ((1, True), (0, False)):
             turn_parts(0, h, left)
+        scale(*steps[0])
+        regroup(*steps[0], 0)
+        for h, left in ((1, True), (0, False)):
             keep_parts(0, h, left)
 
         ride(0, lambda: turn_parts(0, 0, True), lambda: keep_parts(0, 0, True))
         ride(2, lambda: turn_parts(0, 1, False), lambda: keep_parts(0, 1, False))
         ride(4, lambda: turn_row(0, 1), lambda: keep_row(0, 1))
         ride(6, lambda: turn_row(0, 2), lambda: keep_row(0, 2))
-        at = 1
+        at = 2
         for g in range(PASSES):
             for q in range(4):
                 m0 = 4 * q
@@ -444,14 +452,13 @@ def tile_perception_pa_kernel(tc, batch_graph, adj, W1, b1, out):
         for job in (take_root, invert, split):
             after.setdefault(at + 1, []).append(lambda job=job: job(1))
             at += 1
-        at += 3
-        for h, left in ((0, True), (0, False), (1, True), (1, False)):
-            ride(at, lambda h=h, left=left: turn_parts(1, h, left), lambda h=h, left=left: keep_parts(1, h, left))
+        at += 4
+        for job in ((0, True), (0, False), 0, (1, True), (1, False), 1, 2):
+            if isinstance(job, int):
+                ride(at, lambda q=job: turn_row(1, q), lambda q=job: keep_row(1, q))
+            else:
+                ride(at, lambda job=job: turn_parts(1, *job), lambda job=job: keep_parts(1, *job))
             at += 1
-        for q in range(3):
-            ride(at, lambda q=q: turn_row(1, q), lambda q=q: keep_row(1, q))
-            at += 1
-        assert at <= HALFWAY, at
 
         todo = {}
         for k, (b, ib, g) in enumerate(steps):
@@ -463,10 +470,12 @@ def tile_perception_pa_kernel(tc, batch_graph, adj, W1, b1, out):
         for k in range(1, 3):
             factor_bank(*steps[k])
         for k, (b, ib, g) in enumerate(steps):
-            scale(b, ib, g)
+            if k > 0:
+                scale(b, ib, g)
             for job in before.get(k, ()):
                 job()
-            regroup(b, ib, g, k)
+            if k > 0:
+                regroup(b, ib, g, k)
             if k + 3 < N:
                 factor_bank(*steps[k + 3])
             if relus:
@@ -480,7 +489,7 @@ def tile_perception_pa_kernel(tc, batch_graph, adj, W1, b1, out):
                 multiply(*steps[k - 3])
                 if steps[k - 3][2] == PASSES - 1:
                     for m in range(ROW_TILES):
-                        adds.append((k + 2, (*steps[k - 3][:2], m)))
+                        adds.append((k + 3, (*steps[k - 3][:2], m)))
             for step in todo.get(k, ()):
                 twin_factors(*step)
             for job in after.get(k, ()):

@@ -293,10 +293,10 @@ def tile_perception_pa_kernel(tc, batch_graph, adj, W1, b1, out):
         def keep_row(b, q):
             nc.scalar.copy(out=d_row[b][:, K_PASS * q : K_PASS * (q + 1)], in_=banks[b, "row", q][:])
 
-        planes3 = ctx.enter_context(tc.tile_pool(name="planes3", bufs=4))
-        groups3 = ctx.enter_context(tc.tile_pool(name="groups3", bufs=5))
+        planes3 = ctx.enter_context(tc.tile_pool(name="planes3", bufs=5))
+        groups3 = ctx.enter_context(tc.tile_pool(name="groups3", bufs=6))
         factors = ctx.enter_context(tc.tile_pool(name="factors", bufs=3))
-        codes = ctx.enter_context(tc.tile_pool(name="codes", bufs=4))
+        codes = ctx.enter_context(tc.tile_pool(name="codes", bufs=5))
         outs = ctx.enter_context(tc.tile_pool(name="outs", bufs=6))
         a_planes = {}
         a_grouped = {}
@@ -374,7 +374,7 @@ def tile_perception_pa_kernel(tc, batch_graph, adj, W1, b1, out):
             nc.vector.tensor_tensor(out=a_planes[b, ib, g][:], in0=adj_sb[b][g][:, :, i_cols], in1=by, op=ALU.mult)
 
         def on_vector(k):
-            return k % 8 == 3
+            return k % 6 == 3
 
         def regroup(b, ib, g, k):
             a_grouped[b, ib, g] = groups3.tile([P, BLOCK, PACK], BF16, align_bytes=64, name="a_grouped")
@@ -430,10 +430,12 @@ def tile_perception_pa_kernel(tc, batch_graph, adj, W1, b1, out):
         take_root(0)
         invert(0)
         turn_row(0, 0)
+        sum_columns(1, 0, 0, 8)
         keep_row(0, 0)
         split(0)
         for h, left in ((1, True), (0, False)):
             turn_parts(0, h, left)
+        sum_columns(1, 0, 8, 16)
         scale(*steps[0])
         regroup(*steps[0], 0)
         for h, left in ((1, True), (0, False)):
@@ -443,8 +445,8 @@ def tile_perception_pa_kernel(tc, batch_graph, adj, W1, b1, out):
         ride(2, lambda: turn_parts(0, 1, False), lambda: keep_parts(0, 1, False))
         ride(4, lambda: turn_row(0, 1), lambda: keep_row(0, 1))
         ride(6, lambda: turn_row(0, 2), lambda: keep_row(0, 2))
-        at = 2
-        for g in range(PASSES):
+        at = 6
+        for g in range(1, PASSES):
             for q in range(4):
                 m0 = 4 * q
                 ride(at, lambda g=g, m0=m0: sum_columns(1, g, m0, m0 + 4))
@@ -484,17 +486,17 @@ def tile_perception_pa_kernel(tc, batch_graph, adj, W1, b1, out):
                 job = adds.pop(0)[1]
                 add_bias(*job)
                 relus.append(job)
-            if k >= 3:
-                quantise(*steps[k - 3])
-                multiply(*steps[k - 3])
-                if steps[k - 3][2] == PASSES - 1:
+            if k >= 4:
+                quantise(*steps[k - 4])
+                multiply(*steps[k - 4])
+                if steps[k - 4][2] == PASSES - 1:
                     for m in range(ROW_TILES):
-                        adds.append((k + 3, (*steps[k - 3][:2], m)))
+                        adds.append((k + 3, (*steps[k - 4][:2], m)))
             for step in todo.get(k, ()):
                 twin_factors(*step)
             for job in after.get(k, ()):
                 job()
-        for k in range(N - 3, N):
+        for k in range(N - 4, N):
             quantise(*steps[k])
             multiply(*steps[k])
         for at, job in adds:

@@ -39,7 +39,7 @@ def side_by_side(copy, grouped, planes):
 def tile_perception_pa_kernel(tc, batch_graph, adj, W1, b1, out):
     nc = tc.nc
     with ExitStack() as ctx:
-        ctx.enter_context(tc.manual_schedule())
+        ctx.enter_context(tc.manual_schedule(engines={mybir.EngineType.PE}))
         keep = ctx.enter_context(tc.tile_pool(name="keep", bufs=1))
 
         ident = keep.tile([P, P], F32)
@@ -374,7 +374,7 @@ def tile_perception_pa_kernel(tc, batch_graph, adj, W1, b1, out):
             nc.vector.tensor_tensor(out=a_planes[b, ib, g][:], in0=adj_sb[b][g][:, :, i_cols], in1=by, op=ALU.mult)
 
         def on_vector(k):
-            return k % 6 == 3
+            return k % 8 == 3
 
         def regroup(b, ib, g, k):
             a_grouped[b, ib, g] = groups3.tile([P, BLOCK, PACK], BF16, align_bytes=64, name="a_grouped")

from contextlib import ExitStack

import concourse.mybir as mybir
from concourse.masks import make_identity

F32 = mybir.dt.float32
BF16 = mybir.dt.bfloat16
U32 = mybir.dt.uint32
U8 = mybir.dt.uint8
FP8X4 = mybir.dt.float8_e4m3fn_x4
ALU = mybir.AluOpType
ACT = mybir.ActivationFunctionType

P = 128
PACK = 4
K_PASS = P * PACK

GRAPHS, NODES, FEATS, HIDDEN = 2, 2048, 512, 512
CHUNKS = NODES // P
PASSES = NODES // K_PASS
BLOCK = 256
BLOCKS = NODES // BLOCK
ROW_TILES = BLOCK // P
PARTS = 3
LEFT_STEP = 16
TERMS = PARTS * PARTS
HALF = CHUNKS // 2

FLOPS = 2 * GRAPHS * NODES * FEATS * HIDDEN + 2 * GRAPHS * NODES * NODES * HIDDEN


def side_by_side(copy, grouped, planes):
    copy(
        out=grouped.rearrange("p (c i) t -> p c t i", i=4),
        in_=planes.rearrange("p t (c i) -> p c t i", i=4),
    )


def tile_perception_pa_kernel(tc, batch_graph, adj, W1, b1, out):
    nc = tc.nc
    with ExitStack() as ctx:
        ctx.enter_context(tc.manual_schedule(engines={mybir.EngineType.PE}))
        keep = ctx.enter_context(tc.tile_pool(name="keep", bufs=1))

        ident = keep.tile([P, P], F32)
        make_identity(nc, ident[:])
        ident_bf = keep.tile([P, P], BF16)
        make_identity(nc, ident_bf[:])
        ones = keep.tile([P, P], BF16)
        nc.vector.memset(ones[:], 1.0)
        warm = keep.tile([P, 1], F32)
        nc.vector.memset(warm[:], 1.0)
        nc.scalar.activation(out=warm[:], in_=warm[:], func=ACT.Sqrt)

        adj_sb = [
            [keep.tile([P, PACK, NODES], BF16, name="adj%d_%d" % (b, g)) for g in range(PASSES)]
            for b in range(GRAPHS)
        ]
        z_codes = [
            keep.tile([P, PASSES, HIDDEN], U32, align_bytes=64, name="z_codes%d" % b)
            for b in range(GRAPHS)
        ]
        z_scales = [
            keep.tile([P, PASSES, HIDDEN], U8, align_bytes=64, name="z_scales%d" % b)
            for b in range(GRAPHS)
        ]
        d_col = [keep.tile([P, CHUNKS], F32, name="d_col%d" % b) for b in range(GRAPHS)]
        bias_row = keep.tile([P, HIDDEN], F32)

        degrees = ctx.enter_context(tc.psum_pool(name="degrees", bufs=1))
        banks = {}

        def sum_columns(b, g, m0, m1, planes=range(PACK), part=None):
            if (b, "c") not in banks:
                banks[b, "c"] = degrees.tile([P, PASSES + 1, CHUNKS], F32, tag="degrees", name="c_ps")
            for m in range(m0, m1):
                for t in planes:
                    nc.tensor.matmul(
                        out=banks[b, "c"][:, g if part is None else part, m : m + 1],
                        lhsT=adj_sb[b][g][:, t, P * m : P * (m + 1)],
                        rhs=ones[:, 0:1],
                        start=(t == planes[0]),
                        stop=(t == planes[-1]),
                    )

        with ExitStack() as stage1:
            feats = stage1.enter_context(tc.tile_pool(name="feats", bufs=1))
            rows1 = stage1.enter_context(tc.tile_pool(name="rows1", bufs=3))
            work = stage1.enter_context(tc.psum_pool(name="work", bufs=7))

            w_planes = feats.tile([P, PACK, HIDDEN], BF16)
            for u in range(2):
                nc.sync.dma_start(
                    out=w_planes[:, 2 * u : 2 * u + 2, :],
                    in_=W1[256 * u : 256 * u + 256, :].rearrange("(q e) c -> q e c", e=2),
                )
            x_sb = {}
            for b in range(GRAPHS):
                x_chunks = batch_graph[b].rearrange("(r p) k -> p r k", p=P)
                for g in range(PASSES):
                    x_sb[b, g] = feats.tile([P, PACK, FEATS], BF16, name="x%d_%d" % (b, g))
                    nc.sync.dma_start(out=x_sb[b, g][:], in_=x_chunks[:, PACK * g : PACK * (g + 1), :])
            bias_in = feats.tile([P, HIDDEN], BF16)
            nc.vector.memset(bias_in[:], 0.0)
            nc.sync.dma_start(out=bias_in[0:1, :], in_=b1.rearrange("(o h) -> o h", o=1))
            for b in range(GRAPHS):
                adj_chunks = adj[b].rearrange("(r p) i -> p r i", p=P)
                for g in range(PASSES):
                    for t in (0, 2) if (b, g) == (0, PASSES - 1) else (0,):
                        w = 2 if (b, g) == (0, PASSES - 1) else PACK
                        nc.sync.dma_start(
                            out=adj_sb[b][g][:, t : t + w, :], in_=adj_chunks[:, PACK * g + t : PACK * g + t + w, :]
                        )

            w_grouped = feats.tile([P, HIDDEN, PACK], BF16, align_bytes=64)
            side_by_side(nc.vector.tensor_copy, w_grouped[:], w_planes[:])
            w_codes = feats.tile([P, HIDDEN], U32, align_bytes=64)
            w_scales = feats.tile([P, HIDDEN], U8, align_bytes=64)
            nc.vector.quantize_mx(
                out=w_codes[:].bitcast(FP8X4),
                scales=w_scales[:],
                in_=w_grouped[:].rearrange("p c t -> p (c t)"),
            )

            x_codes = {}
            x_scales = {}
            x_grouped = {}
            xt = {}

            def turn_features(b, g):
                x_words = x_sb[b, g][:].bitcast(F32)
                for half in range(2):
                    xt[b, g, half] = work.tile([P, 2, 2, P], F32, tag="work", name="xt")
                    for c in range(2):
                        for u in range(2):
                            nc.tensor.transpose(
                                xt[b, g, half][:, c, u, :],
                                x_words[:, 2 * half + c, P * u : P * (u + 1)],
                                ident[:],
                            )

            def group_features(b, g):
                x_grouped[b, g] = rows1.tile([P, K_PASS, PACK], BF16, align_bytes=64, name="x_grouped")
                words = x_grouped[b, g][:].bitcast(F32)
                for half in range(2):
                    copy = nc.scalar.copy if True else nc.vector.tensor_copy
                    copy(
                        out=words[:, 2 * P * half : 2 * P * (half + 1), :].rearrange("p (c n) u -> p c n u", c=2),
                        in_=xt[b, g, half][:].rearrange("p c u n -> p c n u"),
                    )

            def quantise_features(b, g):
                x_codes[b, g] = rows1.tile([P, K_PASS], U32, align_bytes=64, name="x_codes")
                x_scales[b, g] = rows1.tile([P, K_PASS], U8, align_bytes=64, name="x_scales")
                nc.vector.quantize_mx(
                    out=x_codes[b, g][:].bitcast(FP8X4),
                    scales=x_scales[b, g][:],
                    in_=x_grouped[b, g][:].rearrange("p n t -> p (n t)"),
                )

            z_ps = {}
            z_grouped = {}

            def project(b, g):
                for hb in range(HIDDEN // P):
                    h_cols = slice(P * hb, P * (hb + 1))
                    z_ps[b, g, hb] = work.tile([P, PACK, P], F32, tag="work", name="z_ps")
                    for t in range(PACK):
                        n_cols = slice(P * t, P * (t + 1))
                        nc.tensor.matmul_mx(
                            out=z_ps[b, g, hb][:, t, :],
                            lhsT=x_codes[b, g][:, n_cols].bitcast(FP8X4),
                            lhsT_scale=x_scales[b, g][:, n_cols],
                            rhs=w_codes[:, h_cols].bitcast(FP8X4),
                            rhs_scale=w_scales[:, h_cols],
                            start=True,
                            stop=True,
                        )

            def group_z(b, g):
                z_grouped[b, g] = rows1.tile([P, HIDDEN, PACK], BF16, align_bytes=64, name="z_grouped")
                for hb in range(HIDDEN // P):
                    h_cols = slice(P * hb, P * (hb + 1))
                    copy = nc.vector.tensor_copy if hb % 2 == 0 else nc.scalar.copy
                    copy(out=z_grouped[b, g][:, h_cols, :], in_=z_ps[b, g, hb][:].rearrange("p t h -> p h t"))

            def quantise_z(b, g):
                nc.vector.quantize_mx(
                    out=z_codes[b][:, g, :].bitcast(FP8X4),
                    scales=z_scales[b][:, g, :],
                    in_=z_grouped[b, g][:].rearrange("p h t -> p (h t)"),
                )

            groups = [(b, g) for b in range(GRAPHS) for g in range(PASSES)]
            for n in range(len(groups) + 3):
                if n < len(groups):
                    turn_features(*groups[n])
                    group_features(*groups[n])
                if 1 <= n <= len(groups):
                    quantise_features(*groups[n - 1])
                if 2 <= n < len(groups) + 2:
                    project(*groups[n - 2])
                    group_z(*groups[n - 2])
                if n >= 3:
                    quantise_z(*groups[n - 3])
                if n == 5:
                    bias_ps = work.tile([P, HIDDEN], F32, tag="work")
                    nc.tensor.matmul(out=bias_ps[:], lhsT=ones[:], rhs=bias_in[:], start=True, stop=True)
                    nc.vector.tensor_copy(out=bias_row[:], in_=bias_ps[:])
                g = n - 7
                if 0 <= g < PASSES - 1:
                    sum_columns(0, g, 0, CHUNKS)


        late = ctx.enter_context(tc.tile_pool(name="late", bufs=1))
        d_row = {}
        d_left = {}
        d_right = {}
        left_cols = late.tile([P, CHUNKS * LEFT_STEP + P - LEFT_STEP], BF16)
        right_cols = late.tile([P, CHUNKS, P], BF16)
        nc.gpsimd.memset(left_cols[:], 0.0)
        nc.gpsimd.memset(right_cols[:], 0.0)
        sums = ctx.enter_context(tc.psum_pool(name="sums", bufs=4))
        spread = ctx.enter_context(tc.psum_pool(name="spread", bufs=3))
        c = [keep.tile([P, CHUNKS], F32, name="c%d" % b) for b in range(GRAPHS)]
        root = [keep.tile([P, CHUNKS], F32, name="root%d" % b) for b in range(GRAPHS)]
        rest = [keep.tile([P, CHUNKS], F32, name="rest%d" % b) for b in range(GRAPHS)]
        parts = [keep.tile([P, CHUNKS, PARTS], BF16, name="parts%d" % b) for b in range(GRAPHS)]
        def take_root(b):
            nc.vector.tensor_reduce(
                out=c[b][:],
                in_=banks[b, "c"][:, : PASSES + 1 - b, :].rearrange("p g m -> p m g"),
                axis=mybir.AxisListType.X,
                op=ALU.add,
            )
            nc.scalar.activation(out=root[b][:], in_=c[b][:], func=ACT.Sqrt, bias=1e-30)

        def invert(b):
            nc.vector.reciprocal(out=root[b][:], in_=root[b][:])
            nc.vector.scalar_tensor_tensor(
                out=d_col[b][:], in0=c[b][:], scalar=0.0, in1=root[b][:], op0=ALU.is_gt, op1=ALU.mult
            )

        def split(b):
            eng = nc.vector if b == 0 else nc.gpsimd
            eng.tensor_copy(out=parts[b][:, :, 0], in_=d_col[b][:])
            eng.tensor_sub(out=rest[b][:], in0=d_col[b][:], in1=parts[b][:, :, 0])
            eng.tensor_copy(out=parts[b][:, :, 1], in_=rest[b][:])
            eng.tensor_sub(out=rest[b][:], in0=rest[b][:], in1=parts[b][:, :, 1])
            eng.tensor_copy(out=parts[b][:, :, 2], in_=rest[b][:])
            eng.tensor_copy(
                out=left_cols[:, : CHUNKS * LEFT_STEP]
                .rearrange("p (r k) -> p r k", k=LEFT_STEP)[:, :, :TERMS]
                .rearrange("p r (u v) -> p r u v", v=PARTS),
                in_=parts[b][:].unsqueeze(3).to_broadcast([P, CHUNKS, PARTS, PARTS]),
            )
            eng.tensor_copy(
                out=right_cols[:, :, :TERMS].rearrange("p r (u v) -> p r u v", v=PARTS),
                in_=parts[b][:].unsqueeze(2).to_broadcast([P, CHUNKS, PARTS, PARTS]),
            )

        def turn_parts(b, h, left):
            if b not in d_left:
                d_left[b] = late.tile([P, NODES], BF16, name="d_left", bufs=2)
                d_right[b] = late.tile([P, NODES], BF16, name="d_right", bufs=2)
            pool, tag = (spread, "spread") if b == 0 else (degrees, "degrees")
            bank = pool.tile([P, HALF, P], BF16, tag=tag, name="bank")
            for m in range(HALF):
                r = HALF * h + m
                window = left_cols[:, LEFT_STEP * r : LEFT_STEP * r + P] if left else right_cols[:, r, :]
                nc.tensor.transpose(bank[:, m, :], window, ident_bf[:])
            banks[b, h, left] = bank

        def keep_parts(b, h, left):
            rows = d_left[b] if left else d_right[b]
            nc.scalar.copy(
                out=rows[:, P * HALF * h : P * HALF * (h + 1)], in_=banks[b, h, left][:].rearrange("p m n -> p (m n)")
            )

        def turn_row(b, q):
            if b not in d_row:
                d_row[b] = late.tile([P, 3 * K_PASS], F32, name="d_row")
            pool, tag = (spread, "spread") if b == 0 else (degrees, "degrees")
            banks[b, "row", q] = pool.tile([P, K_PASS], F32, tag=tag, name="d_ps")
            for m in range(PACK):
                r = PACK * q + m
                nc.tensor.transpose(
                    banks[b, "row", q][:, P * m : P * (m + 1)],
                    d_col[b][:, r : r + 1].to_broadcast([P, P]),
                    ident[:],
                )

        def keep_row(b, q):
            nc.scalar.copy(out=d_row[b][:, K_PASS * q : K_PASS * (q + 1)], in_=banks[b, "row", q][:])

        planes3 = ctx.enter_context(tc.tile_pool(name="planes3", bufs=5))
        groups3 = ctx.enter_context(tc.tile_pool(name="groups3", bufs=6))
        factors = ctx.enter_context(tc.tile_pool(name="factors", bufs=3))
        codes = ctx.enter_context(tc.tile_pool(name="codes", bufs=5))
        outs = ctx.enter_context(tc.tile_pool(name="outs", bufs=6))
        a_planes = {}
        a_grouped = {}
        a_codes = {}
        a_scales = {}
        acc = {}
        y = {}
        dd = {}
        twins = ((0, 1), (0, 2), (1, 2), (2, 3))

        def kind(b, ib, g):
            if (b, ib // 2, g) == (0, 0, 0):
                return "row"
            if (ib // 2, g) in twins:
                return "twin"
            if (g, ib // 2) in twins:
                return "mirror"
            return "outer"

        def twin_factors(b, block, g):
            dd[b, block, g] = factors.tile([P, PACK, K_PASS], BF16, name="dd_sb")
            for t in range(PACK):
                r = PACK * g + t
                nc.vector.tensor_scalar_mul(
                    out=dd[b, block, g][:, t, :],
                    in0=d_row[b][:, K_PASS * block : K_PASS * (block + 1)],
                    scalar1=d_col[b][:, r : r + 1],
                )

        def factor_bank(b, ib, g):
            k = kind(b, ib, g)
            if k in ("row", "twin"):
                return
            bank = spread.tile([P, PACK, BLOCK], BF16, tag="spread", name="dd")
            dd[b, ib, g, "bank"] = bank
            for t in range(PACK):
                if k == "mirror":
                    for m in range(ROW_TILES):
                        nc.tensor.transpose(
                            bank[:, t, P * m : P * (m + 1)],
                            dd[b, g, ib // 2][:, ROW_TILES * (ib % 2) + m, P * t : P * (t + 1)],
                            ident_bf[:],
                        )
                else:
                    r = PACK * g + t
                    nc.tensor.matmul(
                        out=bank[:, t, :],
                        lhsT=d_left[b][:, P * r : P * (r + 1)],
                        rhs=d_right[b][:, BLOCK * ib : BLOCK * (ib + 1)],
                        start=True,
                        stop=True,
                    )

        def scale(b, ib, g):
            i_cols = slice(BLOCK * ib, BLOCK * (ib + 1))
            k = kind(b, ib, g)
            a_planes[b, ib, g] = planes3.tile([P, PACK, BLOCK], BF16, name="a_planes")
            if k == "row":
                for t in range(PACK):
                    r = PACK * g + t
                    nc.vector.scalar_tensor_tensor(
                        out=a_planes[b, ib, g][:, t, :],
                        in0=adj_sb[b][g][:, t, i_cols],
                        scalar=d_col[b][:, r : r + 1],
                        in1=d_row[b][:, i_cols],
                        op0=ALU.mult,
                        op1=ALU.mult,
                    )
                return
            if k == "twin":
                half = BLOCK * (ib % 2)
                by = dd[b, ib // 2, g][:, :, half : half + BLOCK]
            else:
                by = dd[b, ib, g, "bank"][:]
            nc.vector.tensor_tensor(out=a_planes[b, ib, g][:], in0=adj_sb[b][g][:, :, i_cols], in1=by, op=ALU.mult)

        def on_vector(k):
            return k % 8 == 3

        def regroup(b, ib, g, k):
            a_grouped[b, ib, g] = groups3.tile([P, BLOCK, PACK], BF16, align_bytes=64, name="a_grouped")
            copy = nc.vector.tensor_copy if on_vector(k) else nc.scalar.copy
            side_by_side(copy, a_grouped[b, ib, g][:], a_planes[b, ib, g][:])

        def quantise(b, ib, g):
            a_codes[b, ib, g] = codes.tile([P, BLOCK], U32, align_bytes=64, name="a_codes")
            a_scales[b, ib, g] = codes.tile([P, BLOCK], U8, align_bytes=64, name="a_scales")
            nc.vector.quantize_mx(
                out=a_codes[b, ib, g][:].bitcast(FP8X4),
                scales=a_scales[b, ib, g][:],
                in_=a_grouped[b, ib, g][:].rearrange("p i t -> p (i t)"),
            )

        def multiply(b, ib, g):
            if g == 0:
                acc[b, ib] = [sums.tile([P, HIDDEN], F32, name="acc%d" % m, tag="acc") for m in range(ROW_TILES)]
            for m in range(ROW_TILES):
                m_cols = slice(P * m, P * (m + 1))
                nc.tensor.matmul_mx(
                    out=acc[b, ib][m][:],
                    lhsT=a_codes[b, ib, g][:, m_cols].bitcast(FP8X4),
                    lhsT_scale=a_scales[b, ib, g][:, m_cols],
                    rhs=z_codes[b][:, g, :].bitcast(FP8X4),
                    rhs_scale=z_scales[b][:, g, :],
                    start=(g == 0),
                    stop=(g == PASSES - 1),
                )

        def add_bias(b, ib, m):
            y[b, ib, m] = outs.tile([P, HIDDEN], F32, name="y")
            nc.vector.tensor_tensor(out=y[b, ib, m][:], in0=acc[b, ib][m][:], in1=bias_row[:], op=ALU.add)

        def rectify(b, ib, m):
            nc.scalar.activation(out=y[b, ib, m][:], in_=y[b, ib, m][:], func=ACT.Relu)
            row0 = BLOCK * ib + P * m
            nc.sync.dma_start(out=out[b, row0 : row0 + P, :], in_=y[b, ib, m][:])

        steps = [(b, ib, g) for b in range(GRAPHS) for ib in range(BLOCKS) for g in range(PASSES)]
        N = len(steps)
        HALFWAY = N // 2
        before = {}
        after = {}

        def ride(at, first, second=None):
            after.setdefault(at, []).append(first)
            if second:
                before.setdefault(at + 1, []).append(second)

        sum_columns(0, PASSES - 1, 0, CHUNKS, range(2))
        sum_columns(0, PASSES - 1, 0, CHUNKS, range(2, PACK), PASSES)
        take_root(0)
        invert(0)
        turn_row(0, 0)
        sum_columns(1, 0, 0, 8)
        keep_row(0, 0)
        split(0)
        for h, left in ((1, True), (0, False)):
            turn_parts(0, h, left)
        sum_columns(1, 0, 8, 16)
        scale(*steps[0])
        regroup(*steps[0], 0)
        for h, left in ((1, True), (0, False)):
            keep_parts(0, h, left)

        ride(0, lambda: turn_parts(0, 0, True), lambda: keep_parts(0, 0, True))
        ride(2, lambda: turn_parts(0, 1, False), lambda: keep_parts(0, 1, False))
        ride(4, lambda: turn_row(0, 1), lambda: keep_row(0, 1))
        ride(6, lambda: turn_row(0, 2), lambda: keep_row(0, 2))
        at = 6
        for g in range(1, PASSES):
            for q in range(4):
                m0 = 4 * q
                ride(at, lambda g=g, m0=m0: sum_columns(1, g, m0, m0 + 4))
                at += 1
        for job in (take_root, invert, split):
            after.setdefault(at + 1, []).append(lambda job=job: job(1))
            at += 1
        at += 4
        for job in ((0, True), (0, False), 0, (1, True), (1, False), 1, 2):
            if isinstance(job, int):
                ride(at, lambda q=job: turn_row(1, q), lambda q=job: keep_row(1, q))
            else:
                ride(at, lambda job=job: turn_parts(1, *job), lambda job=job: keep_parts(1, *job))
            at += 1

        todo = {}
        for k, (b, ib, g) in enumerate(steps):
            if kind(b, ib, g) == "twin" and ib % 2 == 0:
                todo.setdefault(max(k - 3, 0), []).append((b, ib // 2, g))

        adds = []
        relus = []
        for k in range(1, 3):
            factor_bank(*steps[k])
        for k, (b, ib, g) in enumerate(steps):
            if k > 0:
                scale(b, ib, g)
            for job in before.get(k, ()):
                job()
            if k > 0:
                regroup(b, ib, g, k)
            if k + 3 < N:
                factor_bank(*steps[k + 3])
            if relus:
                rectify(*relus.pop(0))
            if adds and k >= adds[0][0]:
                job = adds.pop(0)[1]
                add_bias(*job)
                relus.append(job)
            if k >= 4:
                quantise(*steps[k - 4])
                multiply(*steps[k - 4])
                if steps[k - 4][2] == PASSES - 1:
                    for m in range(ROW_TILES):
                        adds.append((k + 3, (*steps[k - 4][:2], m)))
            for step in todo.get(k, ()):
                twin_factors(*step)
            for job in after.get(k, ()):
                job()
        for k in range(N - 4, N):
            quantise(*steps[k])
            multiply(*steps[k])
        for at, job in adds:
            add_bias(*job)
            relus.append(job)
        for job in relus:
            rectify(*job)
        for m in range(ROW_TILES):
            add_bias(*steps[-1][:2], m)
            rectify(*steps[-1][:2], m)
